import numpy as np
import ml_dtypes


def mxq(x, axis, fmt="e4m3"):
    dtype, down = {"e4m3": (ml_dtypes.float8_e4m3fn, 7), "e5m2": (ml_dtypes.float8_e5m2, 14)}[fmt]
    v = np.moveaxis(np.asarray(x, np.float32).astype(ml_dtypes.bfloat16).astype(np.float64), axis, -1)
    blocks = v.reshape(v.shape[:-1] + (-1, 32))
    amax = np.abs(blocks).max(-1, keepdims=True)
    byte = np.maximum(np.where(amax > 0, np.frexp(amax)[1] - 1 + 127, 0) - down, 1)
    scale = np.exp2(byte - 127.0)
    codes = (blocks / scale).astype(np.float32).astype(dtype).astype(np.float64)
    return np.moveaxis((codes * scale).reshape(v.shape), -1, axis)


WIDE = False


def mx_kscale(k):
    if not WIDE:
        return np.ones(k)
    levels = np.array([10, -10, 5, -5, 0])
    a = np.random.permutation(np.resize(levels, k // 512 * 4)).reshape(k // 512, 4)
    idx = np.arange(k)
    return np.exp2(a[idx // 512, idx % 128 // 32])


BF16 = ml_dtypes.bfloat16


def bf(x):
    return np.asarray(x, np.float32).astype(BF16)


def f64(x):
    return np.asarray(x).astype(np.float64)


E2M1 = np.array([0.0, 0.5, 1.0, 1.5, 2.0, 3.0, 4.0, 6.0, -0.0, -0.5, -1.0, -1.5, -2.0, -3.0, -4.0, -6.0])


def pack_weight(w, fmt):
    k, n = w.shape
    w = f64(bf(w)).reshape(k // 32, 32, n)
    amax = np.abs(w).max(1)
    if fmt == "e4m3":
        byte = np.frexp(amax)[1] - 1 + 127 - 7
    else:
        mant, ex = np.frexp(amax / 6.0)
        byte = np.where(mant > 0.5, ex, ex - 1) + 127
    byte = np.clip(np.where(amax > 0, byte, 1), 1, 254)
    scaled = (w * np.exp2(127.0 - byte)[:, None, :]).reshape(k, n).astype(np.float32)
    by_word = np.ascontiguousarray(scaled.reshape(k // 512, 128, 4, n).transpose(0, 1, 3, 2))
    if fmt == "e4m3":
        words = by_word.astype(ml_dtypes.float8_e4m3fn).view(np.uint8)
    else:
        c = by_word.astype(ml_dtypes.float4_e2m1fn).view(np.uint8) & 0xF
        words = c[..., 0::2] | (c[..., 1::2] << 4)
    return np.ascontiguousarray(words), np.ascontiguousarray(byte.astype(np.uint8).reshape(k // 512, 16, n))


def unpack_weight(words, scales, fmt):
    g, p, n, _ = words.shape
    if fmt == "e4m3":
        vals = np.ascontiguousarray(words).view(ml_dtypes.float8_e4m3fn).astype(np.float64)
    else:
        nib = np.empty((g, p, n, 4), np.uint8)
        nib[..., 0::2] = words & 0xF
        nib[..., 1::2] = words >> 4
        vals = E2M1[nib]
    vals = vals * np.repeat(np.exp2(scales.astype(np.float64) - 127.0), 8, axis=1)[..., None]
    return vals.transpose(0, 1, 3, 2).reshape(g * 512, n)


B, I, H = 512, 1024, 1024
assert H % 512 == 0


def sigmoid(v):
    return 1.0 / (1.0 + np.exp(-v))


def setup_inputs():
    s = mx_kscale(I)
    t = mx_kscale(H)
    x = bf(np.random.standard_normal((B, I)) * s)
    h_tm1 = bf(np.random.standard_normal((B, H)) * t)
    c_tm1 = bf(np.random.standard_normal((B, H)))
    iw_words, iw_scales = pack_weight(np.random.standard_normal((I, 4 * H)) * 0.7 / np.sqrt(I) / s[:, None], "e4m3")
    hw_words, hw_scales = pack_weight(np.random.standard_normal((H, 4 * H)) * 0.7 / np.sqrt(H) / t[:, None], "e4m3")
    bias = bf(np.random.standard_normal(4 * H) * 0.1)
    return {"x": x,
            "h_tm1": h_tm1,
            "c_tm1": c_tm1,
            "input_weight_words": iw_words,
            "input_weight_scales": iw_scales,
            "hidden_state_weight_words": hw_words,
            "hidden_state_weight_scales": hw_scales,
            "bias": bias}


def reference(x, h_tm1, c_tm1, input_weight_words, input_weight_scales, hidden_state_weight_words, hidden_state_weight_scales, bias):
    gx = mxq(f64(x), 1, "e4m3") @ unpack_weight(input_weight_words, input_weight_scales, "e4m3")
    gh = mxq(f64(h_tm1), 1, "e4m3") @ unpack_weight(hidden_state_weight_words, hidden_state_weight_scales, "e4m3")
    gates = gx + gh + f64(bias)
    f_pre, i_pre, c_pre, o_pre = np.split(gates, 4, axis=-1)
    f_t = sigmoid(f_pre)
    i_t = sigmoid(i_pre)
    cand = np.tanh(c_pre)
    c_t = f_t * f64(c_tm1) + i_t * cand
    o_t = sigmoid(o_pre)
    h_t = o_t * np.tanh(c_t)
    return h_t, c_t

@@ -1,0 +1,210 @@
+from contextlib import ExitStack
+
+import concourse.mybir as mybir
+from concourse.masks import make_identity
+
+F32 = mybir.dt.float32
+BF16 = mybir.dt.bfloat16
+I32 = mybir.dt.int32
+U32 = mybir.dt.uint32
+U8 = mybir.dt.uint8
+FP8X4 = mybir.dt.float8_e4m3fn_x4
+SIGMOID = mybir.ActivationFunctionType.Sigmoid
+TANH = mybir.ActivationFunctionType.Tanh
+
+P = 128
+BATCH = 512
+FEATURES = 1024
+FORGET, ENTER, CAND, LEAVE = 0, 1, 2, 3
+GATES = 4
+GATE_FUNC = (SIGMOID, SIGMOID, TANH, SIGMOID)
+GATE_NAME = ("forget", "enter", "cand", "leave")
+SOURCES = 2
+GROUPS = 2
+PASSES = SOURCES * GROUPS
+BANK = 512
+BATCH_TILES = BATCH // P
+HALVES = FEATURES // BANK
+GROUP_WORDS = 256
+
+FLOPS = 2 * BATCH * (SOURCES * FEATURES) * (GATES * FEATURES)
+
+
+def tile_lstmcell_kernel(
+    tc,
+    x,
+    h_tm1,
+    c_tm1,
+    input_weight_words,
+    input_weight_scales,
+    hidden_state_weight_words,
+    hidden_state_weight_scales,
+    bias,
+    out_0,
+    out_1,
+):
+    nc = tc.nc
+    h_t, c_t = out_0, out_1
+    activations = (x, h_tm1)
+    weight_words = (input_weight_words, hidden_state_weight_words)
+    weight_scales = (input_weight_scales, hidden_state_weight_scales)
+
+    with ExitStack() as ctx:
+        keep = ctx.enter_context(tc.tile_pool(name="keep", bufs=1))
+        stage = ctx.enter_context(tc.tile_pool(name="stage", bufs=4))
+        work = ctx.enter_context(tc.tile_pool(name="work", bufs=6))
+        psum = ctx.enter_context(tc.psum_pool(name="psum", bufs=8))
+
+        w_planes = keep.tile([P, PASSES, FEATURES], U8, align_bytes=64)
+        nc.vector.memset(w_planes[:].bitcast(I32), 0)
+        bias_row = keep.tile([P, GATES * FEATURES], BF16)
+        nc.vector.memset(bias_row[:], 0.0)
+        ones = keep.tile([P, P], BF16)
+        nc.vector.memset(ones[:], 1.0)
+        identity = keep.tile([P, P], F32)
+        make_identity(nc, identity[:])
+
+        rows_sb = {}
+
+        def load_activations(src):
+            for m in range(BATCH_TILES):
+                rows_sb[(src, m)] = keep.tile([P, FEATURES], BF16, name="rows%d_%d" % (src, m))
+                nc.sync.dma_start(
+                    out=rows_sb[(src, m)][:], in_=activations[src][m * P : (m + 1) * P, :]
+                )
+
+        def load_scales(src):
+            for g in range(GROUPS):
+                for quadrant in range(4):
+                    nc.sync.dma_start(
+                        out=w_planes[
+                            32 * quadrant : 32 * quadrant + 16, src * GROUPS + g, :
+                        ].bitcast(I32),
+                        in_=weight_scales[src]
+                        .bitcast(I32)[g, 4 * quadrant : 4 * quadrant + 4, :]
+                        .rearrange("r (j n) -> j r n", j=GATES),
+                    )
+
+        w_words = {}
+
+        def load_weights(src, gate, half):
+            first = gate * FEATURES + half * BANK
+            w_words[(src, gate, half)] = keep.tile(
+                [P, GROUPS, BANK], U32, name="w%d_%d_%d" % (src, gate, half), align_bytes=64
+            )
+            nc.sync.dma_start(
+                out=w_words[(src, gate, half)][:].bitcast(I32),
+                in_=weight_words[src]
+                .rearrange("g p n t -> p g (n t)")
+                .bitcast(I32)[:, :, first : first + BANK],
+            )
+
+        load_activations(0)
+        nc.sync.dma_start(out=bias_row[0:1, :], in_=bias.unsqueeze(0))
+        load_scales(0)
+        load_weights(0, FORGET, 0)
+        load_activations(1)
+        load_scales(1)
+        load_weights(1, FORGET, 0)
+        c_prev = {}
+        for m in range(BATCH_TILES):
+            c_prev[m] = keep.tile([P, FEATURES], BF16, name="c_prev%d" % m)
+            nc.sync.dma_start(out=c_prev[m][:], in_=c_tm1[m * P : (m + 1) * P, :])
+        for half in range(HALVES):
+            for gate in range(GATES):
+                if (gate, half) != (FORGET, 0):
+                    load_weights(0, gate, half)
+                    load_weights(1, gate, half)
+
+        a_codes = {}
+        a_scales = {}
+        for src in range(SOURCES):
+            a_codes[src] = keep.tile(
+                [P, BATCH_TILES, GROUPS, P], U32, name="a_codes%d" % src, align_bytes=64
+            )
+            a_scales[src] = keep.tile(
+                [P, BATCH_TILES, GROUPS, P], U8, name="a_scales%d" % src, align_bytes=64
+            )
+            for m in range(BATCH_TILES):
+                words = rows_sb[(src, m)][:].bitcast(F32)
+                flipped = psum.tile([P, GROUPS, 2, P], F32, tag="bank")
+                for g in range(GROUPS):
+                    for u in range(2):
+                        nc.tensor.transpose(
+                            flipped[:, g, u, :],
+                            words[:, g * GROUP_WORDS + u : (g + 1) * GROUP_WORDS : 2],
+                            identity[:],
+                        )
+                grouped = stage.tile([P, GROUPS * P * 4], BF16, align_bytes=64)
+                nc.scalar.copy(
+                    out=grouped[:].bitcast(F32).rearrange("p (g b u) -> p g b u", g=GROUPS, u=2),
+                    in_=flipped[:].rearrange("p g u b -> p g b u"),
+                )
+                nc.vector.quantize_mx(
+                    out=a_codes[src][:, m, :, :].rearrange("p g b -> p (g b)").bitcast(FP8X4),
+                    scales=a_scales[src][:, m, :, :].rearrange("p g b -> p (g b)"),
+                    in_=grouped[:],
+                )
+
+        bias_all = keep.tile([P, GATES * FEATURES], F32)
+        for j in range(GATES * HALVES):
+            spread = psum.tile([P, BANK], F32, tag="bank")
+            nc.tensor.matmul(
+                spread[:],
+                lhsT=ones[:],
+                rhs=bias_row[:, j * BANK : (j + 1) * BANK],
+                start=True,
+                stop=True,
+            )
+            nc.vector.tensor_copy(out=bias_all[:, j * BANK : (j + 1) * BANK], in_=spread[:])
+
+        def mx_pass(acc, m, gate, half, k):
+            src, g = divmod(k, GROUPS)
+            nc.tensor.matmul_mx(
+                out=acc[:],
+                lhsT=a_codes[src][:, m, g, :].bitcast(FP8X4),
+                lhsT_scale=a_scales[src][:, m, g, :],
+                rhs=w_words[(src, gate, half)][:, g, :].bitcast(FP8X4),
+                rhs_scale=w_planes[4 * gate : P, k, half * BANK : (half + 1) * BANK],
+                start=(k == 0),
+                stop=(k == PASSES - 1),
+            )
+
+        gate_sb = {}
+        tanh_c = {}
+
+        def finish_gate(acc, m, gate, half):
+            first = gate * FEATURES + half * BANK
+            value = work.tile([P, BANK], F32, tag=GATE_NAME[gate])
+            nc.vector.tensor_add(out=value[:], in0=acc[:], in1=bias_all[:, first : first + BANK])
+            nc.scalar.activation(out=value[:], in_=value[:], func=GATE_FUNC[gate])
+            gate_sb[(m, gate)] = value
+            rows = slice(m * P, (m + 1) * P)
+            cols = slice(half * BANK, (half + 1) * BANK)
+            if gate == FORGET:
+                nc.vector.tensor_mul(out=value[:], in0=value[:], in1=c_prev[m][:, cols])
+            if gate == CAND:
+                nc.vector.tensor_mul(out=value[:], in0=value[:], in1=gate_sb[(m, ENTER)][:])
+                c_new = work.tile([P, BANK], F32)
+                nc.vector.tensor_add(out=c_new[:], in0=value[:], in1=gate_sb[(m, FORGET)][:])
+                nc.sync.dma_start(out=c_t[rows, cols], in_=c_new[:])
+                tanh_c[m] = work.tile([P, BANK], F32, name="tanh_c")
+                nc.scalar.activation(out=tanh_c[m][:], in_=c_new[:], func=TANH)
+            if gate == LEAVE:
+                h_new = work.tile([P, BANK], F32)
+                nc.vector.tensor_mul(out=h_new[:], in0=value[:], in1=tanh_c[m][:])
+                nc.sync.dma_start(out=h_t[rows, cols], in_=h_new[:])
+
+        for gate in range(GATES):
+            accs = [psum.tile([P, BANK], F32, name="acc", tag="bank") for m in range(BATCH_TILES)]
+            for k in range(PASSES):
+                for m in range(BATCH_TILES):
+                    mx_pass(accs[m], m, gate, 0, k)
+            for m in range(BATCH_TILES):
+                finish_gate(accs[m], m, gate, 0)
+        for m in range(BATCH_TILES):
+            for gate in range(GATES):
+                acc = psum.tile([P, BANK], F32, tag="bank")
+                for k in range(PASSES):
+                    mx_pass(acc, m, gate, 1, k)
+                finish_gate(acc, m, gate, 1)

@@ -182,9 +182,9 @@ def tile_lstmcell_kernel(
             rows = slice(m * P, (m + 1) * P)
             cols = slice(half * BANK, (half + 1) * BANK)
             if gate == FORGET:
-                nc.vector.tensor_mul(out=value[:], in0=value[:], in1=c_prev[m][:, cols])
+                nc.gpsimd.tensor_mul(out=value[:], in0=value[:], in1=c_prev[m][:, cols])
             if gate == CAND:
-                nc.vector.tensor_mul(out=value[:], in0=value[:], in1=gate_sb[(m, ENTER)][:])
+                nc.gpsimd.tensor_mul(out=value[:], in0=value[:], in1=gate_sb[(m, ENTER)][:])
                 c_new = work.tile([P, BANK], F32)
                 nc.vector.tensor_add(out=c_new[:], in0=value[:], in1=gate_sb[(m, FORGET)][:])
                 nc.sync.dma_start(out=c_t[rows, cols], in_=c_new[:])

@@ -54,6 +54,7 @@ def tile_lstmcell_kernel(
         stage = ctx.enter_context(tc.tile_pool(name="stage", bufs=4))
         work = ctx.enter_context(tc.tile_pool(name="work", bufs=6))
         psum = ctx.enter_context(tc.psum_pool(name="psum", bufs=8))
+        ctx.enter_context(tc.manual_schedule())
 
         w_planes = keep.tile([P, PASSES, FEATURES], U8, align_bytes=64)
         nc.vector.memset(w_planes[:].bitcast(I32), 0)
@@ -63,6 +64,9 @@ def tile_lstmcell_kernel(
         nc.vector.memset(ones[:], 1.0)
         identity = keep.tile([P, P], F32)
         make_identity(nc, identity[:])
+        table_warmer = keep.tile([P, 1], F32)
+        nc.vector.memset(table_warmer[:], 0.0)
+        nc.scalar.activation(out=table_warmer[:], in_=table_warmer[:], func=SIGMOID)
 
         rows_sb = {}
 
@@ -99,6 +103,15 @@ def tile_lstmcell_kernel(
                 .bitcast(I32)[:, :, first : first + BANK],
             )
 
+        c_prev = {}
+
+        def load_cell(half):
+            c_prev[half] = keep.tile([P, BATCH_TILES, BANK], BF16, name="c_prev%d" % half)
+            nc.sync.dma_start(
+                out=c_prev[half][:],
+                in_=c_tm1[:, half * BANK : (half + 1) * BANK].rearrange("(m p) c -> p m c", p=P),
+            )
+
         load_activations(0)
         nc.sync.dma_start(out=bias_row[0:1, :], in_=bias.unsqueeze(0))
         load_scales(0)
@@ -106,19 +119,19 @@ def tile_lstmcell_kernel(
         load_activations(1)
         load_scales(1)
         load_weights(1, FORGET, 0)
-        c_prev = {}
-        for m in range(BATCH_TILES):
-            c_prev[m] = keep.tile([P, FEATURES], BF16, name="c_prev%d" % m)
-            nc.sync.dma_start(out=c_prev[m][:], in_=c_tm1[m * P : (m + 1) * P, :])
-        for half in range(HALVES):
-            for gate in range(GATES):
-                if (gate, half) != (FORGET, 0):
-                    load_weights(0, gate, half)
-                    load_weights(1, gate, half)
+        load_cell(0)
+        for gate in (ENTER, CAND, LEAVE):
+            load_weights(0, gate, 0)
+            load_weights(1, gate, 0)
+        load_cell(1)
+        for gate in range(GATES):
+            load_weights(0, gate, 1)
+            load_weights(1, gate, 1)
 
         a_codes = {}
         a_scales = {}
-        for src in range(SOURCES):
+
+        def quantise_activations(src):
             a_codes[src] = keep.tile(
                 [P, BATCH_TILES, GROUPS, P], U32, name="a_codes%d" % src, align_bytes=64
             )
@@ -146,17 +159,24 @@ def tile_lstmcell_kernel(
                     in_=grouped[:],
                 )
 
+        quantise_activations(0)
+
         bias_all = keep.tile([P, GATES * FEATURES], F32)
-        for j in range(GATES * HALVES):
-            spread = psum.tile([P, BANK], F32, tag="bank")
-            nc.tensor.matmul(
-                spread[:],
-                lhsT=ones[:],
-                rhs=bias_row[:, j * BANK : (j + 1) * BANK],
-                start=True,
-                stop=True,
-            )
-            nc.vector.tensor_copy(out=bias_all[:, j * BANK : (j + 1) * BANK], in_=spread[:])
+        for half in range(HALVES):
+            for gate in range(GATES):
+                first = gate * FEATURES + half * BANK
+                spread = psum.tile([P, BANK], F32, tag="bank")
+                nc.tensor.matmul(
+                    spread[:],
+                    lhsT=ones[:],
+                    rhs=bias_row[:, first : first + BANK],
+                    start=True,
+                    stop=True,
+                )
+                if half == 0:
+                    nc.scalar.copy(out=bias_all[:, first : first + BANK], in_=spread[:])
+                else:
+                    nc.vector.tensor_copy(out=bias_all[:, first : first + BANK], in_=spread[:])
 
         def mx_pass(acc, m, gate, half, k):
             src, g = divmod(k, GROUPS)
@@ -173,38 +193,61 @@ def tile_lstmcell_kernel(
         gate_sb = {}
         tanh_c = {}
 
-        def finish_gate(acc, m, gate, half):
+        def activate(acc, m, gate, half):
             first = gate * FEATURES + half * BANK
             value = work.tile([P, BANK], F32, tag=GATE_NAME[gate])
             nc.vector.tensor_add(out=value[:], in0=acc[:], in1=bias_all[:, first : first + BANK])
             nc.scalar.activation(out=value[:], in_=value[:], func=GATE_FUNC[gate])
-            gate_sb[(m, gate)] = value
-            rows = slice(m * P, (m + 1) * P)
-            cols = slice(half * BANK, (half + 1) * BANK)
+            gate_sb[(m, gate, half)] = value
+
+        def cell_state(m, gate, half):
+            value = gate_sb[(m, gate, half)]
             if gate == FORGET:
-                nc.gpsimd.tensor_mul(out=value[:], in0=value[:], in1=c_prev[m][:, cols])
+                nc.vector.tensor_mul(out=value[:], in0=value[:], in1=c_prev[half][:, m, :])
             if gate == CAND:
-                nc.gpsimd.tensor_mul(out=value[:], in0=value[:], in1=gate_sb[(m, ENTER)][:])
+                nc.vector.tensor_mul(out=value[:], in0=value[:], in1=gate_sb[(m, ENTER, half)][:])
                 c_new = work.tile([P, BANK], F32)
-                nc.vector.tensor_add(out=c_new[:], in0=value[:], in1=gate_sb[(m, FORGET)][:])
-                nc.sync.dma_start(out=c_t[rows, cols], in_=c_new[:])
-                tanh_c[m] = work.tile([P, BANK], F32, name="tanh_c")
-                nc.scalar.activation(out=tanh_c[m][:], in_=c_new[:], func=TANH)
+                nc.vector.tensor_add(out=c_new[:], in0=value[:], in1=gate_sb[(m, FORGET, half)][:])
+                nc.sync.dma_start(
+                    out=c_t[m * P : (m + 1) * P, half * BANK : (half + 1) * BANK], in_=c_new[:]
+                )
+                tanh_c[(m, half)] = work.tile([P, BANK], F32, name="tanh_c")
+                nc.scalar.activation(out=tanh_c[(m, half)][:], in_=c_new[:], func=TANH)
+
+        def cell_output(m, gate, half):
             if gate == LEAVE:
                 h_new = work.tile([P, BANK], F32)
-                nc.vector.tensor_mul(out=h_new[:], in0=value[:], in1=tanh_c[m][:])
-                nc.sync.dma_start(out=h_t[rows, cols], in_=h_new[:])
+                nc.vector.tensor_mul(
+                    out=h_new[:], in0=gate_sb[(m, LEAVE, half)][:], in1=tanh_c[(m, half)][:]
+                )
+                nc.sync.dma_start(
+                    out=h_t[m * P : (m + 1) * P, half * BANK : (half + 1) * BANK], in_=h_new[:]
+                )
 
-        for gate in range(GATES):
-            accs = [psum.tile([P, BANK], F32, name="acc", tag="bank") for m in range(BATCH_TILES)]
-            for k in range(PASSES):
-                for m in range(BATCH_TILES):
-                    mx_pass(accs[m], m, gate, 0, k)
-            for m in range(BATCH_TILES):
-                finish_gate(accs[m], m, gate, 0)
+        pieces = [(m, gate, 0) for gate in range(GATES) for m in range(BATCH_TILES)]
+        pieces.extend([(m, gate, 1) for m in range(BATCH_TILES) for gate in range(GATES)])
+
+        early = {}
         for m in range(BATCH_TILES):
-            for gate in range(GATES):
-                acc = psum.tile([P, BANK], F32, tag="bank")
-                for k in range(PASSES):
-                    mx_pass(acc, m, gate, 1, k)
-                finish_gate(acc, m, gate, 1)
+            early[m] = psum.tile([P, BANK], F32, name="acc", tag="bank")
+        for k in range(GROUPS):
+            for m in range(BATCH_TILES):
+                mx_pass(early[m], m, FORGET, 0, k)
+        quantise_activations(1)
+
+        for j in range(len(pieces) + 2):
+            if j < len(pieces):
+                m, gate, half = pieces[j]
+                if j < BATCH_TILES:
+                    acc = early[m]
+                    passes_done = GROUPS
+                else:
+                    acc = psum.tile([P, BANK], F32, tag="bank")
+                    passes_done = 0
+                for k in range(passes_done, PASSES):
+                    mx_pass(acc, m, gate, half, k)
+                activate(acc, m, gate, half)
+            if 1 <= j <= len(pieces):
+                cell_state(*pieces[j - 1])
+            if j >= 2:
+                cell_output(*pieces[j - 2])

@@ -26,6 +26,8 @@ BANK = 512
 BATCH_TILES = BATCH // P
 HALVES = FEATURES // BANK
 GROUP_WORDS = 256
+STATE_LAG = 2
+OUTPUT_LAG = 3
 
 FLOPS = 2 * BATCH * (SOURCES * FEATURES) * (GATES * FEATURES)
 
@@ -58,12 +60,12 @@ def tile_lstmcell_kernel(
 
         w_planes = keep.tile([P, PASSES, FEATURES], U8, align_bytes=64)
         nc.vector.memset(w_planes[:].bitcast(I32), 0)
-        bias_row = keep.tile([P, GATES * FEATURES], BF16)
-        nc.vector.memset(bias_row[:], 0.0)
-        ones = keep.tile([P, P], BF16)
-        nc.vector.memset(ones[:], 1.0)
+        bias_rows = keep.tile([P, BANK], BF16)
+        nc.vector.memset(bias_rows[:], 0.0)
         identity = keep.tile([P, P], F32)
         make_identity(nc, identity[:])
+        identity_bf = keep.tile([P, P], BF16)
+        make_identity(nc, identity_bf[:])
         table_warmer = keep.tile([P, 1], F32)
         nc.vector.memset(table_warmer[:], 0.0)
         nc.scalar.activation(out=table_warmer[:], in_=table_warmer[:], func=SIGMOID)
@@ -113,10 +115,12 @@ def tile_lstmcell_kernel(
             )
 
         load_activations(0)
-        nc.sync.dma_start(out=bias_row[0:1, :], in_=bias.unsqueeze(0))
+        nc.sync.dma_start(
+            out=bias_rows[0 : GATES * HALVES, :], in_=bias.rearrange("(j n) -> j n", n=BANK)
+        )
+        load_activations(1)
         load_scales(0)
         load_weights(0, FORGET, 0)
-        load_activations(1)
         load_scales(1)
         load_weights(1, FORGET, 0)
         load_cell(0)
@@ -159,24 +163,24 @@ def tile_lstmcell_kernel(
                     in_=grouped[:],
                 )
 
-        quantise_activations(0)
-
         bias_all = keep.tile([P, GATES * FEATURES], F32)
-        for half in range(HALVES):
+
+        def spread_bias(half):
             for gate in range(GATES):
-                first = gate * FEATURES + half * BANK
+                j = gate * HALVES + half
                 spread = psum.tile([P, BANK], F32, tag="bank")
                 nc.tensor.matmul(
                     spread[:],
-                    lhsT=ones[:],
-                    rhs=bias_row[:, first : first + BANK],
+                    lhsT=identity_bf[:, j : j + 1].to_broadcast([P, P]),
+                    rhs=bias_rows[:],
                     start=True,
                     stop=True,
                 )
-                if half == 0:
-                    nc.scalar.copy(out=bias_all[:, first : first + BANK], in_=spread[:])
-                else:
-                    nc.vector.tensor_copy(out=bias_all[:, first : first + BANK], in_=spread[:])
+                nc.scalar.copy(out=bias_all[:, j * BANK : (j + 1) * BANK], in_=spread[:])
+
+        quantise_activations(0)
+        spread_bias(0)
+        quantise_activations(1)
 
         def mx_pass(acc, m, gate, half, k):
             src, g = divmod(k, GROUPS)
@@ -224,8 +228,11 @@ def tile_lstmcell_kernel(
                     out=h_t[m * P : (m + 1) * P, half * BANK : (half + 1) * BANK], in_=h_new[:]
                 )
 
-        pieces = [(m, gate, 0) for gate in range(GATES) for m in range(BATCH_TILES)]
-        pieces.extend([(m, gate, 1) for m in range(BATCH_TILES) for gate in range(GATES)])
+        pieces = [(m, FORGET, 0) for m in range(BATCH_TILES)]
+        pieces.extend([(m, gate, 0) for m in range(BATCH_TILES) for gate in (ENTER, CAND)])
+        pieces.extend([(m, LEAVE, 0) for m in range(BATCH_TILES)])
+        pieces.extend([(m, gate, 1) for m in range(BATCH_TILES) for gate in (FORGET, ENTER, CAND)])
+        pieces.extend([(m, LEAVE, 1) for m in range(BATCH_TILES)])
 
         early = {}
         for m in range(BATCH_TILES):
@@ -233,9 +240,10 @@ def tile_lstmcell_kernel(
         for k in range(GROUPS):
             for m in range(BATCH_TILES):
                 mx_pass(early[m], m, FORGET, 0, k)
-        quantise_activations(1)
 
-        for j in range(len(pieces) + 2):
+        for j in range(len(pieces) + OUTPUT_LAG):
+            if j == BATCH_TILES:
+                spread_bias(1)
             if j < len(pieces):
                 m, gate, half = pieces[j]
                 if j < BATCH_TILES:
@@ -247,7 +255,7 @@ def tile_lstmcell_kernel(
                 for k in range(passes_done, PASSES):
                     mx_pass(acc, m, gate, half, k)
                 activate(acc, m, gate, half)
-            if 1 <= j <= len(pieces):
-                cell_state(*pieces[j - 1])
-            if j >= 2:
-                cell_output(*pieces[j - 2])
+            if STATE_LAG <= j < len(pieces) + STATE_LAG:
+                cell_state(*pieces[j - STATE_LAG])
+            if j >= OUTPUT_LAG:
+                cell_output(*pieces[j - OUTPUT_LAG])

@@ -210,6 +210,10 @@ def tile_lstmcell_kernel(
                 nc.vector.tensor_mul(out=value[:], in0=value[:], in1=c_prev[half][:, m, :])
             if gate == CAND:
                 nc.vector.tensor_mul(out=value[:], in0=value[:], in1=gate_sb[(m, ENTER, half)][:])
+
+        def cell_sum(m, gate, half):
+            value = gate_sb[(m, gate, half)]
+            if gate == CAND:
                 c_new = work.tile([P, BANK], F32)
                 nc.vector.tensor_add(out=c_new[:], in0=value[:], in1=gate_sb[(m, FORGET, half)][:])
                 nc.sync.dma_start(
@@ -258,4 +262,5 @@ def tile_lstmcell_kernel(
             if STATE_LAG <= j < len(pieces) + STATE_LAG:
                 cell_state(*pieces[j - STATE_LAG])
             if j >= OUTPUT_LAG:
+                cell_sum(*pieces[j - OUTPUT_LAG])
                 cell_output(*pieces[j - OUTPUT_LAG])

@@ -26,25 +26,16 @@ BANK = 512
 BATCH_TILES = BATCH // P
 HALVES = FEATURES // BANK
 GROUP_WORDS = 256
+PLANE_ROWS = 4
 STATE_LAG = 2
 OUTPUT_LAG = 3
+LATE_BIAS = False
 
 FLOPS = 2 * BATCH * (SOURCES * FEATURES) * (GATES * FEATURES)
 
 
-def tile_lstmcell_kernel(
-    tc,
-    x,
-    h_tm1,
-    c_tm1,
-    input_weight_words,
-    input_weight_scales,
-    hidden_state_weight_words,
-    hidden_state_weight_scales,
-    bias,
-    out_0,
-    out_1,
-):
+def tile_lstmcell_kernel(tc, x, h_tm1, c_tm1, input_weight_words, input_weight_scales,
+                                       hidden_state_weight_words, hidden_state_weight_scales, bias, out_0, out_1):
     nc = tc.nc
     h_t, c_t = out_0, out_1
     activations = (x, h_tm1)
@@ -60,10 +51,10 @@ def tile_lstmcell_kernel(
 
         w_planes = keep.tile([P, PASSES, FEATURES], U8, align_bytes=64)
         nc.vector.memset(w_planes[:].bitcast(I32), 0)
-        bias_rows = keep.tile([P, BANK], BF16)
-        nc.vector.memset(bias_rows[:], 0.0)
         identity = keep.tile([P, P], F32)
         make_identity(nc, identity[:])
+        bias_rows = keep.tile([P, BANK], BF16)
+        nc.gpsimd.memset(bias_rows[:], 0.0)
         identity_bf = keep.tile([P, P], BF16)
         make_identity(nc, identity_bf[:])
         table_warmer = keep.tile([P, 1], F32)
@@ -71,38 +62,30 @@ def tile_lstmcell_kernel(
         nc.scalar.activation(out=table_warmer[:], in_=table_warmer[:], func=SIGMOID)
 
         rows_sb = {}
+        for src in range(SOURCES):
+            rows_sb[src] = keep.tile([P, BATCH_TILES, FEATURES], BF16, name="rows%d" % src)
 
-        def load_activations(src):
-            for m in range(BATCH_TILES):
-                rows_sb[(src, m)] = keep.tile([P, FEATURES], BF16, name="rows%d_%d" % (src, m))
+        def load_activations(src, first, count):
+            nc.sync.dma_start(
+                out=rows_sb[src][:, first : first + count, :],
+                in_=activations[src][first * P : (first + count) * P, :].rearrange("(m p) k -> p m k", p=P),
+            )
+
+        def load_scales(src, g):
+            for quadrant in range(4):
                 nc.sync.dma_start(
-                    out=rows_sb[(src, m)][:], in_=activations[src][m * P : (m + 1) * P, :]
+                    out=w_planes[32 * quadrant : 32 * quadrant + 16, src * GROUPS + g, :].bitcast(I32),
+                    in_=weight_scales[src].bitcast(I32)[g, 4 * quadrant : 4 * quadrant + 4, :].rearrange("r (j n) -> j r n", j=GATES),
                 )
-
-        def load_scales(src):
-            for g in range(GROUPS):
-                for quadrant in range(4):
-                    nc.sync.dma_start(
-                        out=w_planes[
-                            32 * quadrant : 32 * quadrant + 16, src * GROUPS + g, :
-                        ].bitcast(I32),
-                        in_=weight_scales[src]
-                        .bitcast(I32)[g, 4 * quadrant : 4 * quadrant + 4, :]
-                        .rearrange("r (j n) -> j r n", j=GATES),
-                    )
 
         w_words = {}
 
         def load_weights(src, gate, half):
             first = gate * FEATURES + half * BANK
-            w_words[(src, gate, half)] = keep.tile(
-                [P, GROUPS, BANK], U32, name="w%d_%d_%d" % (src, gate, half), align_bytes=64
-            )
+            w_words[(src, gate, half)] = keep.tile([P, GROUPS, BANK], U32, name="w%d_%d_%d" % (src, gate, half), align_bytes=64)
             nc.sync.dma_start(
                 out=w_words[(src, gate, half)][:].bitcast(I32),
-                in_=weight_words[src]
-                .rearrange("g p n t -> p g (n t)")
-                .bitcast(I32)[:, :, first : first + BANK],
+                in_=weight_words[src].rearrange("g p n t -> p g (n t)").bitcast(I32)[:, :, first : first + BANK],
             )
 
         c_prev = {}
@@ -114,14 +97,24 @@ def tile_lstmcell_kernel(
                 in_=c_tm1[:, half * BANK : (half + 1) * BANK].rearrange("(m p) c -> p m c", p=P),
             )
 
-        load_activations(0)
-        nc.sync.dma_start(
-            out=bias_rows[0 : GATES * HALVES, :], in_=bias.rearrange("(j n) -> j n", n=BANK)
-        )
-        load_activations(1)
-        load_scales(0)
+        bias_all = keep.tile([P, HALVES, GATES, BANK], F32)
+
+        def spread_bias(gate, half):
+            j = gate * HALVES + half
+            spread = psum.tile([P, BANK], F32, name="spread", tag="bank")
+            nc.tensor.matmul(spread[:], lhsT=identity_bf[:, j : j + 1].to_broadcast([P, P]), rhs=bias_rows[:], start=True, stop=True)
+            nc.scalar.copy(out=bias_all[:, half, gate, :], in_=spread[:])
+
+        load_activations(0, 0, 2)
+        load_scales(0, 0)
+        load_activations(0, 2, 2)
+        nc.gpsimd.dma_start(out=bias_rows[0 : GATES * HALVES, :], in_=bias.rearrange("(j n) -> j n", n=BANK))
+        load_scales(0, 1)
         load_weights(0, FORGET, 0)
-        load_scales(1)
+        load_activations(1, 0, 2)
+        load_scales(1, 0)
+        load_activations(1, 2, 2)
+        load_scales(1, 1)
         load_weights(1, FORGET, 0)
         load_cell(0)
         for gate in (ENTER, CAND, LEAVE):
@@ -134,62 +127,46 @@ def tile_lstmcell_kernel(
 
         a_codes = {}
         a_scales = {}
+        for src in range(SOURCES):
+            a_codes[src] = keep.tile([P, BATCH_TILES, GROUPS, P], U32, name="a_codes%d" % src, align_bytes=64)
+            a_scales[src] = keep.tile([P, BATCH_TILES, GROUPS, P], U8, name="a_scales%d" % src, align_bytes=64)
 
-        def quantise_activations(src):
-            a_codes[src] = keep.tile(
-                [P, BATCH_TILES, GROUPS, P], U32, name="a_codes%d" % src, align_bytes=64
+        flipped = {}
+        grouped = {}
+
+        def flip(src, m):
+            words = rows_sb[src][:, m, :].bitcast(F32)
+            flipped[(src, m)] = psum.tile([P, GROUPS, 2, P], F32, name="flipped", tag="bank")
+            for g in range(GROUPS):
+                for u in range(2):
+                    nc.tensor.transpose(flipped[(src, m)][:, g, u, :], words[:, g * GROUP_WORDS + u : (g + 1) * GROUP_WORDS : 2], identity[:])
+
+        def regroup(src, m, engine):
+            grouped[(src, m)] = stage.tile([P, GROUPS * P * 4], BF16, name="grouped", align_bytes=64)
+            out = grouped[(src, m)][:].bitcast(F32).rearrange("p (g b u) -> p g b u", g=GROUPS, u=2)
+            in_ = flipped[(src, m)][:].rearrange("p g u b -> p g b u")
+            if engine == 0:
+                nc.scalar.copy(out=out, in_=in_)
+            else:
+                nc.vector.tensor_copy(out=out, in_=in_)
+
+        def quantise(src, m):
+            nc.vector.quantize_mx(
+                out=a_codes[src][:, m, :, :].rearrange("p g b -> p (g b)").bitcast(FP8X4),
+                scales=a_scales[src][:, m, :, :].rearrange("p g b -> p (g b)"),
+                in_=grouped[(src, m)][:],
             )
-            a_scales[src] = keep.tile(
-                [P, BATCH_TILES, GROUPS, P], U8, name="a_scales%d" % src, align_bytes=64
-            )
-            for m in range(BATCH_TILES):
-                words = rows_sb[(src, m)][:].bitcast(F32)
-                flipped = psum.tile([P, GROUPS, 2, P], F32, tag="bank")
-                for g in range(GROUPS):
-                    for u in range(2):
-                        nc.tensor.transpose(
-                            flipped[:, g, u, :],
-                            words[:, g * GROUP_WORDS + u : (g + 1) * GROUP_WORDS : 2],
-                            identity[:],
-                        )
-                grouped = stage.tile([P, GROUPS * P * 4], BF16, align_bytes=64)
-                nc.scalar.copy(
-                    out=grouped[:].bitcast(F32).rearrange("p (g b u) -> p g b u", g=GROUPS, u=2),
-                    in_=flipped[:].rearrange("p g u b -> p g b u"),
-                )
-                nc.vector.quantize_mx(
-                    out=a_codes[src][:, m, :, :].rearrange("p g b -> p (g b)").bitcast(FP8X4),
-                    scales=a_scales[src][:, m, :, :].rearrange("p g b -> p (g b)"),
-                    in_=grouped[:],
-                )
 
-        bias_all = keep.tile([P, GATES * FEATURES], F32)
-
-        def spread_bias(half):
-            for gate in range(GATES):
-                j = gate * HALVES + half
-                spread = psum.tile([P, BANK], F32, tag="bank")
-                nc.tensor.matmul(
-                    spread[:],
-                    lhsT=identity_bf[:, j : j + 1].to_broadcast([P, P]),
-                    rhs=bias_rows[:],
-                    start=True,
-                    stop=True,
-                )
-                nc.scalar.copy(out=bias_all[:, j * BANK : (j + 1) * BANK], in_=spread[:])
-
-        quantise_activations(0)
-        spread_bias(0)
-        quantise_activations(1)
 
         def mx_pass(acc, m, gate, half, k):
             src, g = divmod(k, GROUPS)
+            first = gate * FEATURES + half * BANK
             nc.tensor.matmul_mx(
                 out=acc[:],
                 lhsT=a_codes[src][:, m, g, :].bitcast(FP8X4),
                 lhsT_scale=a_scales[src][:, m, g, :],
                 rhs=w_words[(src, gate, half)][:, g, :].bitcast(FP8X4),
-                rhs_scale=w_planes[4 * gate : P, k, half * BANK : (half + 1) * BANK],
+                rhs_scale=w_planes[PLANE_ROWS * gate : P, k, half * BANK : (half + 1) * BANK],
                 start=(k == 0),
                 stop=(k == PASSES - 1),
             )
@@ -198,9 +175,8 @@ def tile_lstmcell_kernel(
         tanh_c = {}
 
         def activate(acc, m, gate, half):
-            first = gate * FEATURES + half * BANK
-            value = work.tile([P, BANK], F32, tag=GATE_NAME[gate])
-            nc.vector.tensor_add(out=value[:], in0=acc[:], in1=bias_all[:, first : first + BANK])
+            value = work.tile([P, BANK], F32, name="value", tag=GATE_NAME[gate])
+            nc.vector.tensor_add(out=value[:], in0=acc[:], in1=bias_all[:, half, gate, :])
             nc.scalar.activation(out=value[:], in_=value[:], func=GATE_FUNC[gate])
             gate_sb[(m, gate, half)] = value
 
@@ -214,23 +190,17 @@ def tile_lstmcell_kernel(
         def cell_sum(m, gate, half):
             value = gate_sb[(m, gate, half)]
             if gate == CAND:
-                c_new = work.tile([P, BANK], F32)
+                c_new = work.tile([P, BANK], F32, name="c_new")
                 nc.vector.tensor_add(out=c_new[:], in0=value[:], in1=gate_sb[(m, FORGET, half)][:])
-                nc.sync.dma_start(
-                    out=c_t[m * P : (m + 1) * P, half * BANK : (half + 1) * BANK], in_=c_new[:]
-                )
+                nc.sync.dma_start(out=c_t[m * P : (m + 1) * P, half * BANK : (half + 1) * BANK], in_=c_new[:])
                 tanh_c[(m, half)] = work.tile([P, BANK], F32, name="tanh_c")
                 nc.scalar.activation(out=tanh_c[(m, half)][:], in_=c_new[:], func=TANH)
 
         def cell_output(m, gate, half):
             if gate == LEAVE:
-                h_new = work.tile([P, BANK], F32)
-                nc.vector.tensor_mul(
-                    out=h_new[:], in0=gate_sb[(m, LEAVE, half)][:], in1=tanh_c[(m, half)][:]
-                )
-                nc.sync.dma_start(
-                    out=h_t[m * P : (m + 1) * P, half * BANK : (half + 1) * BANK], in_=h_new[:]
-                )
+                h_new = work.tile([P, BANK], F32, name="h_new")
+                nc.vector.tensor_mul(out=h_new[:], in0=gate_sb[(m, LEAVE, half)][:], in1=tanh_c[(m, half)][:])
+                nc.sync.dma_start(out=h_t[m * P : (m + 1) * P, half * BANK : (half + 1) * BANK], in_=h_new[:])
 
         pieces = [(m, FORGET, 0) for m in range(BATCH_TILES)]
         pieces.extend([(m, gate, 0) for m in range(BATCH_TILES) for gate in (ENTER, CAND)])
@@ -239,22 +209,42 @@ def tile_lstmcell_kernel(
         pieces.extend([(m, LEAVE, 1) for m in range(BATCH_TILES)])
 
         early = {}
+        flip(0, 0)
+        regroup(0, 0, 0)
+        flip(0, 1)
+        regroup(0, 1, 1)
+        quantise(0, 0)
+        quantise(0, 1)
+        for gate in range(GATES):
+            spread_bias(gate, 0)
+        flip(0, 2)
+        regroup(0, 2, 1)
+        flip(0, 3)
+        regroup(0, 3, 0)
+        quantise(0, 2)
+        quantise(0, 3)
+        for gate in range(GATES):
+            spread_bias(gate, 1)
         for m in range(BATCH_TILES):
             early[m] = psum.tile([P, BANK], F32, name="acc", tag="bank")
-        for k in range(GROUPS):
-            for m in range(BATCH_TILES):
+            for k in range(GROUPS):
                 mx_pass(early[m], m, FORGET, 0, k)
+        for m in range(BATCH_TILES):
+            flip(1, m)
+            regroup(1, m, 0)
+            quantise(1, m)
 
         for j in range(len(pieces) + OUTPUT_LAG):
-            if j == BATCH_TILES:
-                spread_bias(1)
+            if j == BATCH_TILES and LATE_BIAS:
+                for gate in range(GATES):
+                    spread_bias(gate, 1)
             if j < len(pieces):
                 m, gate, half = pieces[j]
-                if j < BATCH_TILES:
+                if j < len(early):
                     acc = early[m]
                     passes_done = GROUPS
                 else:
-                    acc = psum.tile([P, BANK], F32, tag="bank")
+                    acc = psum.tile([P, BANK], F32, name="acc", tag="bank")
                     passes_done = 0
                 for k in range(passes_done, PASSES):
                     mx_pass(acc, m, gate, half, k)

@@ -51,10 +51,10 @@ def tile_lstmcell_kernel(tc, x, h_tm1, c_tm1, input_weight_words, input_weight_s
 
         w_planes = keep.tile([P, PASSES, FEATURES], U8, align_bytes=64)
         nc.vector.memset(w_planes[:].bitcast(I32), 0)
-        identity = keep.tile([P, P], F32)
-        make_identity(nc, identity[:])
         bias_rows = keep.tile([P, BANK], BF16)
         nc.gpsimd.memset(bias_rows[:], 0.0)
+        identity = keep.tile([P, P], F32)
+        make_identity(nc, identity[:])
         identity_bf = keep.tile([P, P], BF16)
         make_identity(nc, identity_bf[:])
         table_warmer = keep.tile([P, 1], F32)
@@ -99,16 +99,25 @@ def tile_lstmcell_kernel(tc, x, h_tm1, c_tm1, input_weight_words, input_weight_s
 
         bias_all = keep.tile([P, HALVES, GATES, BANK], F32)
 
-        def spread_bias(gate, half):
+        spread = {}
+
+        def spread_bias(n):
+            half, gate = divmod(n, GATES)
             j = gate * HALVES + half
-            spread = psum.tile([P, BANK], F32, name="spread", tag="bank")
-            nc.tensor.matmul(spread[:], lhsT=identity_bf[:, j : j + 1].to_broadcast([P, P]), rhs=bias_rows[:], start=True, stop=True)
-            nc.scalar.copy(out=bias_all[:, half, gate, :], in_=spread[:])
+            spread[n] = psum.tile([P, BANK], F32, name="spread", tag="bank")
+            nc.tensor.matmul(spread[n][:], lhsT=identity_bf[:, j : j + 1].to_broadcast([P, P]), rhs=bias_rows[:], start=True, stop=True)
+
+        def keep_bias(n, engine):
+            half, gate = divmod(n, GATES)
+            if engine == 0:
+                nc.scalar.copy(out=bias_all[:, half, gate, :], in_=spread[n][:])
+            else:
+                nc.vector.tensor_copy(out=bias_all[:, half, gate, :], in_=spread[n][:])
 
         load_activations(0, 0, 2)
+        nc.sync.dma_start(out=bias_rows[0 : GATES * HALVES, :], in_=bias.rearrange("(j n) -> j n", n=BANK))
         load_scales(0, 0)
         load_activations(0, 2, 2)
-        nc.gpsimd.dma_start(out=bias_rows[0 : GATES * HALVES, :], in_=bias.rearrange("(j n) -> j n", n=BANK))
         load_scales(0, 1)
         load_weights(0, FORGET, 0)
         load_activations(1, 0, 2)
@@ -215,29 +224,49 @@ def tile_lstmcell_kernel(tc, x, h_tm1, c_tm1, input_weight_words, input_weight_s
         regroup(0, 1, 1)
         quantise(0, 0)
         quantise(0, 1)
-        for gate in range(GATES):
-            spread_bias(gate, 0)
+        spread_bias(0)
+        spread_bias(1)
+        spread_bias(2)
+        keep_bias(0, 0)
+        keep_bias(1, 0)
         flip(0, 2)
-        regroup(0, 2, 1)
+        regroup(0, 2, 0)
         flip(0, 3)
-        regroup(0, 3, 0)
+        regroup(0, 3, 1)
         quantise(0, 2)
         quantise(0, 3)
-        for gate in range(GATES):
-            spread_bias(gate, 1)
+        keep_bias(2, 0)
+        for n in range(3, 8):
+            spread_bias(n)
+        keep_bias(3, 0)
+        keep_bias(4, 0)
+        keep_bias(5, 0)
+        keep_bias(6, 1)
+        keep_bias(7, 1)
         for m in range(BATCH_TILES):
             early[m] = psum.tile([P, BANK], F32, name="acc", tag="bank")
-            for k in range(GROUPS):
-                mx_pass(early[m], m, FORGET, 0, k)
-        for m in range(BATCH_TILES):
-            flip(1, m)
-            regroup(1, m, 0)
-            quantise(1, m)
+        for k in range(GROUPS):
+            mx_pass(early[0], 0, FORGET, 0, k)
+        for k in range(GROUPS):
+            mx_pass(early[1], 1, FORGET, 0, k)
+        flip(1, 0)
+        regroup(1, 0, 0)
+        quantise(1, 0)
+        flip(1, 1)
+        regroup(1, 1, 0)
+        quantise(1, 1)
+        flip(1, 2)
+        regroup(1, 2, 0)
+        quantise(1, 2)
+        flip(1, 3)
+        regroup(1, 3, 0)
+        quantise(1, 3)
+        for k in range(GROUPS):
+            mx_pass(early[2], 2, FORGET, 0, k)
+        for k in range(GROUPS):
+            mx_pass(early[3], 3, FORGET, 0, k)
 
         for j in range(len(pieces) + OUTPUT_LAG):
-            if j == BATCH_TILES and LATE_BIAS:
-                for gate in range(GATES):
-                    spread_bias(gate, 1)
             if j < len(pieces):
                 m, gate, half = pieces[j]
                 if j < len(early):

@@ -49,7 +49,7 @@ def tile_lstmcell_kernel(tc, x, h_tm1, c_tm1, input_weight_words, input_weight_s
         psum = ctx.enter_context(tc.psum_pool(name="psum", bufs=8))
         ctx.enter_context(tc.manual_schedule())
 
-        w_planes = keep.tile([P, PASSES, FEATURES], U8, align_bytes=64)
+        w_planes = keep.tile([P, PASSES, FEATURES], U8, align_bytes=256)
         nc.vector.memset(w_planes[:].bitcast(I32), 0)
         bias_rows = keep.tile([P, BANK], BF16)
         nc.gpsimd.memset(bias_rows[:], 0.0)
@@ -82,7 +82,7 @@ def tile_lstmcell_kernel(tc, x, h_tm1, c_tm1, input_weight_words, input_weight_s
 
         def load_weights(src, gate, half):
             first = gate * FEATURES + half * BANK
-            w_words[(src, gate, half)] = keep.tile([P, GROUPS, BANK], U32, name="w%d_%d_%d" % (src, gate, half), align_bytes=64)
+            w_words[(src, gate, half)] = keep.tile([P, GROUPS, BANK], U32, name="w%d_%d_%d" % (src, gate, half), align_bytes=256)
             nc.sync.dma_start(
                 out=w_words[(src, gate, half)][:].bitcast(I32),
                 in_=weight_words[src].rearrange("g p n t -> p g (n t)").bitcast(I32)[:, :, first : first + BANK],
@@ -137,8 +137,8 @@ def tile_lstmcell_kernel(tc, x, h_tm1, c_tm1, input_weight_words, input_weight_s
         a_codes = {}
         a_scales = {}
         for src in range(SOURCES):
-            a_codes[src] = keep.tile([P, BATCH_TILES, GROUPS, P], U32, name="a_codes%d" % src, align_bytes=64)
-            a_scales[src] = keep.tile([P, BATCH_TILES, GROUPS, P], U8, name="a_scales%d" % src, align_bytes=64)
+            a_codes[src] = keep.tile([P, BATCH_TILES, GROUPS, P], U32, name="a_codes%d" % src, align_bytes=256)
+            a_scales[src] = keep.tile([P, BATCH_TILES, GROUPS, P], U8, name="a_scales%d" % src, align_bytes=256)
 
         flipped = {}
         grouped = {}
@@ -151,7 +151,7 @@ def tile_lstmcell_kernel(tc, x, h_tm1, c_tm1, input_weight_words, input_weight_s
                     nc.tensor.transpose(flipped[(src, m)][:, g, u, :], words[:, g * GROUP_WORDS + u : (g + 1) * GROUP_WORDS : 2], identity[:])
 
         def regroup(src, m, engine):
-            grouped[(src, m)] = stage.tile([P, GROUPS * P * 4], BF16, name="grouped", align_bytes=64)
+            grouped[(src, m)] = stage.tile([P, GROUPS * P * 4], BF16, name="grouped", align_bytes=256)
             out = grouped[(src, m)][:].bitcast(F32).rearrange("p (g b u) -> p g b u", g=GROUPS, u=2)
             in_ = flipped[(src, m)][:].rearrange("p g u b -> p g b u")
             if engine == 0:

@@ -11,6 +11,8 @@ U8 = mybir.dt.uint8
 FP8X4 = mybir.dt.float8_e4m3fn_x4
 SIGMOID = mybir.ActivationFunctionType.Sigmoid
 TANH = mybir.ActivationFunctionType.Tanh
+MULT = mybir.AluOpType.mult
+ADD = mybir.AluOpType.add
 
 P = 128
 BATCH = 512
@@ -27,9 +29,6 @@ BATCH_TILES = BATCH // P
 HALVES = FEATURES // BANK
 GROUP_WORDS = 256
 PLANE_ROWS = 4
-STATE_LAG = 2
-OUTPUT_LAG = 3
-LATE_BIAS = False
 
 FLOPS = 2 * BATCH * (SOURCES * FEATURES) * (GATES * FEATURES)
 
@@ -51,12 +50,8 @@ def tile_lstmcell_kernel(tc, x, h_tm1, c_tm1, input_weight_words, input_weight_s
 
         w_planes = keep.tile([P, PASSES, FEATURES], U8, align_bytes=256)
         nc.vector.memset(w_planes[:].bitcast(I32), 0)
-        bias_rows = keep.tile([P, BANK], BF16)
-        nc.gpsimd.memset(bias_rows[:], 0.0)
         identity = keep.tile([P, P], F32)
         make_identity(nc, identity[:])
-        identity_bf = keep.tile([P, P], BF16)
-        make_identity(nc, identity_bf[:])
         table_warmer = keep.tile([P, 1], F32)
         nc.vector.memset(table_warmer[:], 0.0)
         nc.scalar.activation(out=table_warmer[:], in_=table_warmer[:], func=SIGMOID)
@@ -97,25 +92,13 @@ def tile_lstmcell_kernel(tc, x, h_tm1, c_tm1, input_weight_words, input_weight_s
                 in_=c_tm1[:, half * BANK : (half + 1) * BANK].rearrange("(m p) c -> p m c", p=P),
             )
 
-        bias_all = keep.tile([P, HALVES, GATES, BANK], F32)
+        bias_all = keep.tile([P, HALVES, GATES, BANK], BF16)
 
-        spread = {}
-
-        def spread_bias(n):
-            half, gate = divmod(n, GATES)
-            j = gate * HALVES + half
-            spread[n] = psum.tile([P, BANK], F32, name="spread", tag="bank")
-            nc.tensor.matmul(spread[n][:], lhsT=identity_bf[:, j : j + 1].to_broadcast([P, P]), rhs=bias_rows[:], start=True, stop=True)
-
-        def keep_bias(n, engine):
-            half, gate = divmod(n, GATES)
-            if engine == 0:
-                nc.scalar.copy(out=bias_all[:, half, gate, :], in_=spread[n][:])
-            else:
-                nc.vector.tensor_copy(out=bias_all[:, half, gate, :], in_=spread[n][:])
+        def load_bias(gate, half):
+            first = gate * FEATURES + half * BANK
+            nc.sync.dma_start(out=bias_all[:, half, gate, :], in_=bias[first : first + BANK].partition_broadcast(P))
 
         load_activations(0, 0, 2)
-        nc.sync.dma_start(out=bias_rows[0 : GATES * HALVES, :], in_=bias.rearrange("(j n) -> j n", n=BANK))
         load_scales(0, 0)
         load_activations(0, 2, 2)
         load_scales(0, 1)
@@ -125,14 +108,18 @@ def tile_lstmcell_kernel(tc, x, h_tm1, c_tm1, input_weight_words, input_weight_s
         load_activations(1, 2, 2)
         load_scales(1, 1)
         load_weights(1, FORGET, 0)
-        load_cell(0)
+        load_bias(FORGET, 0)
         for gate in (ENTER, CAND, LEAVE):
             load_weights(0, gate, 0)
             load_weights(1, gate, 0)
+            load_bias(gate, 0)
+            if gate == ENTER:
+                load_cell(0)
         load_cell(1)
         for gate in range(GATES):
             load_weights(0, gate, 1)
             load_weights(1, gate, 1)
+            load_bias(gate, 1)
 
         a_codes = {}
         a_scales = {}
@@ -189,30 +176,37 @@ def tile_lstmcell_kernel(tc, x, h_tm1, c_tm1, input_weight_words, input_weight_s
             nc.scalar.activation(out=value[:], in_=value[:], func=GATE_FUNC[gate])
             gate_sb[(m, gate, half)] = value
 
-        def cell_state(m, gate, half):
-            value = gate_sb[(m, gate, half)]
-            if gate == FORGET:
-                nc.vector.tensor_mul(out=value[:], in0=value[:], in1=c_prev[half][:, m, :])
-            if gate == CAND:
-                nc.vector.tensor_mul(out=value[:], in0=value[:], in1=gate_sb[(m, ENTER, half)][:])
+        def forget_times_cell(m, half):
+            value = gate_sb[(m, FORGET, half)]
+            nc.gpsimd.tensor_tensor(out=value[:], in0=value[:], in1=c_prev[half][:, m, :], op=MULT)
 
-        def cell_sum(m, gate, half):
-            value = gate_sb[(m, gate, half)]
-            if gate == CAND:
-                c_new = work.tile([P, BANK], F32, name="c_new")
-                nc.vector.tensor_add(out=c_new[:], in0=value[:], in1=gate_sb[(m, FORGET, half)][:])
-                nc.sync.dma_start(out=c_t[m * P : (m + 1) * P, half * BANK : (half + 1) * BANK], in_=c_new[:])
-                tanh_c[(m, half)] = work.tile([P, BANK], F32, name="tanh_c")
-                nc.scalar.activation(out=tanh_c[(m, half)][:], in_=c_new[:], func=TANH)
+        def enter_times_cand(m, half):
+            value = gate_sb[(m, CAND, half)]
+            nc.vector.tensor_mul(out=value[:], in0=value[:], in1=gate_sb[(m, ENTER, half)][:])
 
-        def cell_output(m, gate, half):
-            if gate == LEAVE:
-                h_new = work.tile([P, BANK], F32, name="h_new")
-                nc.vector.tensor_mul(out=h_new[:], in0=gate_sb[(m, LEAVE, half)][:], in1=tanh_c[(m, half)][:])
-                nc.sync.dma_start(out=h_t[m * P : (m + 1) * P, half * BANK : (half + 1) * BANK], in_=h_new[:])
+        c_sb = {}
+
+        def cell_sum(m, half, on_vector):
+            c_new = work.tile([P, BANK], F32, name="c_new")
+            c_sb[(m, half)] = c_new
+            if on_vector:
+                nc.vector.tensor_add(out=c_new[:], in0=gate_sb[(m, CAND, half)][:], in1=gate_sb[(m, FORGET, half)][:])
+            else:
+                nc.gpsimd.tensor_tensor(out=c_new[:], in0=gate_sb[(m, CAND, half)][:], in1=gate_sb[(m, FORGET, half)][:], op=ADD)
+            nc.sync.dma_start(out=c_t[m * P : (m + 1) * P, half * BANK : (half + 1) * BANK], in_=c_new[:])
+
+        def cell_tanh(m, half):
+            tanh_c[(m, half)] = work.tile([P, BANK], F32, name="tanh_c")
+            nc.scalar.activation(out=tanh_c[(m, half)][:], in_=c_sb[(m, half)][:], func=TANH)
+
+        def cell_output(m, half):
+            h_new = work.tile([P, BANK], F32, name="h_new")
+            nc.vector.tensor_mul(out=h_new[:], in0=gate_sb[(m, LEAVE, half)][:], in1=tanh_c[(m, half)][:])
+            nc.sync.dma_start(out=h_t[m * P : (m + 1) * P, half * BANK : (half + 1) * BANK], in_=h_new[:])
 
         pieces = [(m, FORGET, 0) for m in range(BATCH_TILES)]
-        pieces.extend([(m, gate, 0) for m in range(BATCH_TILES) for gate in (ENTER, CAND)])
+        pieces.extend([(m, ENTER, 0) for m in range(BATCH_TILES)])
+        pieces.extend([(m, CAND, 0) for m in range(BATCH_TILES)])
         pieces.extend([(m, LEAVE, 0) for m in range(BATCH_TILES)])
         pieces.extend([(m, gate, 1) for m in range(BATCH_TILES) for gate in (FORGET, ENTER, CAND)])
         pieces.extend([(m, LEAVE, 1) for m in range(BATCH_TILES)])
@@ -224,25 +218,12 @@ def tile_lstmcell_kernel(tc, x, h_tm1, c_tm1, input_weight_words, input_weight_s
         regroup(0, 1, 1)
         quantise(0, 0)
         quantise(0, 1)
-        spread_bias(0)
-        spread_bias(1)
-        spread_bias(2)
-        keep_bias(0, 0)
-        keep_bias(1, 0)
         flip(0, 2)
         regroup(0, 2, 0)
         flip(0, 3)
         regroup(0, 3, 1)
         quantise(0, 2)
         quantise(0, 3)
-        keep_bias(2, 0)
-        for n in range(3, 8):
-            spread_bias(n)
-        keep_bias(3, 0)
-        keep_bias(4, 0)
-        keep_bias(5, 0)
-        keep_bias(6, 1)
-        keep_bias(7, 1)
         for m in range(BATCH_TILES):
             early[m] = psum.tile([P, BANK], F32, name="acc", tag="bank")
         for k in range(GROUPS):
@@ -266,7 +247,13 @@ def tile_lstmcell_kernel(tc, x, h_tm1, c_tm1, input_weight_words, input_weight_s
         for k in range(GROUPS):
             mx_pass(early[3], 3, FORGET, 0, k)
 
-        for j in range(len(pieces) + OUTPUT_LAG):
+        later = {}
+        tanh_step = {}
+
+        def at(step, action, *args):
+            later.setdefault(step, []).append((action, args))
+
+        for j in range(len(pieces) + 4):
             if j < len(pieces):
                 m, gate, half = pieces[j]
                 if j < len(early):
@@ -278,8 +265,20 @@ def tile_lstmcell_kernel(tc, x, h_tm1, c_tm1, input_weight_words, input_weight_s
                 for k in range(passes_done, PASSES):
                     mx_pass(acc, m, gate, half, k)
                 activate(acc, m, gate, half)
-            if STATE_LAG <= j < len(pieces) + STATE_LAG:
-                cell_state(*pieces[j - STATE_LAG])
-            if j >= OUTPUT_LAG:
-                cell_sum(*pieces[j - OUTPUT_LAG])
-                cell_output(*pieces[j - OUTPUT_LAG])
+                last_cell = (m == BATCH_TILES - 1 and half == HALVES - 1)
+                if gate == FORGET:
+                    at(j + 2, forget_times_cell, m, half)
+                if gate == CAND and last_cell:
+                    at(j + 1, enter_times_cand, m, half)
+                    at(j + 2, cell_sum, m, half, True)
+                    tanh_step[(m, half)] = j + 3
+                    at(tanh_step[(m, half)], cell_tanh, m, half)
+                elif gate == CAND:
+                    at(j + 2, enter_times_cand, m, half)
+                    at(j + 3, cell_sum, m, half, False)
+                    tanh_step[(m, half)] = j + 5
+                    at(tanh_step[(m, half)], cell_tanh, m, half)
+                if gate == LEAVE:
+                    at(max(j, tanh_step[(m, half)]) + 2, cell_output, m, half)
+            for action, args in later.get(j, []):
+                action(*args)

@@ -50,6 +50,10 @@ def tile_lstmcell_kernel(tc, x, h_tm1, c_tm1, input_weight_words, input_weight_s
 
         w_planes = keep.tile([P, PASSES, FEATURES], U8, align_bytes=256)
         nc.vector.memset(w_planes[:].bitcast(I32), 0)
+        bias_rows = keep.tile([P, BANK], BF16)
+        nc.gpsimd.memset(bias_rows[:], 0.0)
+        identity_bf = keep.tile([P, P], BF16)
+        make_identity(nc, identity_bf[:])
         identity = keep.tile([P, P], F32)
         make_identity(nc, identity[:])
         table_warmer = keep.tile([P, 1], F32)
@@ -92,12 +96,24 @@ def tile_lstmcell_kernel(tc, x, h_tm1, c_tm1, input_weight_words, input_weight_s
                 in_=c_tm1[:, half * BANK : (half + 1) * BANK].rearrange("(m p) c -> p m c", p=P),
             )
 
-        bias_all = keep.tile([P, HALVES, GATES, BANK], BF16)
+        bias_all = keep.tile([P, HALVES, GATES, BANK], F32)
 
-        def load_bias(gate, half):
-            first = gate * FEATURES + half * BANK
-            nc.sync.dma_start(out=bias_all[:, half, gate, :], in_=bias[first : first + BANK].partition_broadcast(P))
+        spread = {}
 
+        def spread_bias(n):
+            half, gate = divmod(n, GATES)
+            j = gate * HALVES + half
+            spread[n] = psum.tile([P, BANK], F32, name="spread", tag="bank")
+            nc.tensor.matmul(spread[n][:], lhsT=identity_bf[:, j : j + 1].to_broadcast([P, P]), rhs=bias_rows[:], start=True, stop=True)
+
+        def keep_bias(n, engine):
+            half, gate = divmod(n, GATES)
+            if engine == 0:
+                nc.scalar.copy(out=bias_all[:, half, gate, :], in_=spread[n][:])
+            else:
+                nc.vector.tensor_copy(out=bias_all[:, half, gate, :], in_=spread[n][:])
+
+        nc.sync.dma_start(out=bias_rows[0 : GATES * HALVES, :], in_=bias.rearrange("(j n) -> j n", n=BANK))
         load_activations(0, 0, 2)
         load_scales(0, 0)
         load_activations(0, 2, 2)
@@ -108,18 +124,15 @@ def tile_lstmcell_kernel(tc, x, h_tm1, c_tm1, input_weight_words, input_weight_s
         load_activations(1, 2, 2)
         load_scales(1, 1)
         load_weights(1, FORGET, 0)
-        load_bias(FORGET, 0)
         for gate in (ENTER, CAND, LEAVE):
             load_weights(0, gate, 0)
             load_weights(1, gate, 0)
-            load_bias(gate, 0)
             if gate == ENTER:
                 load_cell(0)
         load_cell(1)
         for gate in range(GATES):
             load_weights(0, gate, 1)
             load_weights(1, gate, 1)
-            load_bias(gate, 1)
 
         a_codes = {}
         a_scales = {}
@@ -212,18 +225,32 @@ def tile_lstmcell_kernel(tc, x, h_tm1, c_tm1, input_weight_words, input_weight_s
         pieces.extend([(m, LEAVE, 1) for m in range(BATCH_TILES)])
 
         early = {}
+        for n in range(4):
+            spread_bias(n)
+        keep_bias(0, 0)
+        keep_bias(1, 1)
+        keep_bias(2, 0)
+        keep_bias(3, 1)
         flip(0, 0)
         regroup(0, 0, 0)
         flip(0, 1)
         regroup(0, 1, 1)
         quantise(0, 0)
         quantise(0, 1)
+        spread_bias(4)
+        spread_bias(5)
         flip(0, 2)
         regroup(0, 2, 0)
         flip(0, 3)
         regroup(0, 3, 1)
         quantise(0, 2)
         quantise(0, 3)
+        keep_bias(4, 0)
+        keep_bias(5, 0)
+        spread_bias(6)
+        spread_bias(7)
+        keep_bias(6, 0)
+        keep_bias(7, 0)
         for m in range(BATCH_TILES):
             early[m] = psum.tile([P, BANK], F32, name="acc", tag="bank")
         for k in range(GROUPS):

@@ -113,8 +113,8 @@ def tile_lstmcell_kernel(tc, x, h_tm1, c_tm1, input_weight_words, input_weight_s
             else:
                 nc.vector.tensor_copy(out=bias_all[:, half, gate, :], in_=spread[n][:])
 
-        nc.sync.dma_start(out=bias_rows[0 : GATES * HALVES, :], in_=bias.rearrange("(j n) -> j n", n=BANK))
         load_activations(0, 0, 2)
+        nc.sync.dma_start(out=bias_rows[0 : GATES * HALVES, :], in_=bias.rearrange("(j n) -> j n", n=BANK))
         load_scales(0, 0)
         load_activations(0, 2, 2)
         load_scales(0, 1)
@@ -221,36 +221,36 @@ def tile_lstmcell_kernel(tc, x, h_tm1, c_tm1, input_weight_words, input_weight_s
         pieces.extend([(m, ENTER, 0) for m in range(BATCH_TILES)])
         pieces.extend([(m, CAND, 0) for m in range(BATCH_TILES)])
         pieces.extend([(m, LEAVE, 0) for m in range(BATCH_TILES)])
-        pieces.extend([(m, gate, 1) for m in range(BATCH_TILES) for gate in (FORGET, ENTER, CAND)])
+        pieces.extend([(m, FORGET, 1) for m in range(BATCH_TILES)])
+        pieces.extend([(m, gate, 1) for m in range(BATCH_TILES) for gate in (ENTER, CAND)])
         pieces.extend([(m, LEAVE, 1) for m in range(BATCH_TILES)])
 
         early = {}
-        for n in range(4):
-            spread_bias(n)
-        keep_bias(0, 0)
-        keep_bias(1, 1)
-        keep_bias(2, 0)
-        keep_bias(3, 1)
         flip(0, 0)
         regroup(0, 0, 0)
         flip(0, 1)
         regroup(0, 1, 1)
         quantise(0, 0)
         quantise(0, 1)
-        spread_bias(4)
-        spread_bias(5)
+        spread_bias(0)
+        spread_bias(1)
+        spread_bias(2)
+        keep_bias(0, 0)
+        keep_bias(1, 0)
         flip(0, 2)
         regroup(0, 2, 0)
         flip(0, 3)
         regroup(0, 3, 1)
         quantise(0, 2)
         quantise(0, 3)
+        keep_bias(2, 0)
+        for n in range(3, 8):
+            spread_bias(n)
+        keep_bias(3, 0)
         keep_bias(4, 0)
         keep_bias(5, 0)
-        spread_bias(6)
-        spread_bias(7)
-        keep_bias(6, 0)
-        keep_bias(7, 0)
+        keep_bias(6, 1)
+        keep_bias(7, 1)
         for m in range(BATCH_TILES):
             early[m] = psum.tile([P, BANK], F32, name="acc", tag="bank")
         for k in range(GROUPS):
@@ -292,7 +292,7 @@ def tile_lstmcell_kernel(tc, x, h_tm1, c_tm1, input_weight_words, input_weight_s
                 for k in range(passes_done, PASSES):
                     mx_pass(acc, m, gate, half, k)
                 activate(acc, m, gate, half)
-                last_cell = (m == BATCH_TILES - 1 and half == HALVES - 1)
+                last_cell = (m >= BATCH_TILES - 2 and half == HALVES - 1)
                 if gate == FORGET:
                     at(j + 2, forget_times_cell, m, half)
                 if gate == CAND and last_cell:

@@ -45,7 +45,8 @@ def tile_lstmcell_kernel(tc, x, h_tm1, c_tm1, input_weight_words, input_weight_s
         keep = ctx.enter_context(tc.tile_pool(name="keep", bufs=1))
         stage = ctx.enter_context(tc.tile_pool(name="stage", bufs=4))
         work = ctx.enter_context(tc.tile_pool(name="work", bufs=6))
-        psum = ctx.enter_context(tc.psum_pool(name="psum", bufs=8))
+        psum_a = ctx.enter_context(tc.psum_pool(name="psum_a", bufs=4))
+        psum_b = ctx.enter_context(tc.psum_pool(name="psum_b", bufs=4))
         ctx.enter_context(tc.manual_schedule())
 
         w_planes = keep.tile([P, PASSES, FEATURES], U8, align_bytes=256)
@@ -70,11 +71,11 @@ def tile_lstmcell_kernel(tc, x, h_tm1, c_tm1, input_weight_words, input_weight_s
                 in_=activations[src][first * P : (first + count) * P, :].rearrange("(m p) k -> p m k", p=P),
             )
 
-        def load_scales(src, g):
+        def load_scales(src, g, half):
             for quadrant in range(4):
                 nc.sync.dma_start(
-                    out=w_planes[32 * quadrant : 32 * quadrant + 16, src * GROUPS + g, :].bitcast(I32),
-                    in_=weight_scales[src].bitcast(I32)[g, 4 * quadrant : 4 * quadrant + 4, :].rearrange("r (j n) -> j r n", j=GATES),
+                    out=w_planes[32 * quadrant : 32 * quadrant + 16, src * GROUPS + g, half * BANK : (half + 1) * BANK].bitcast(I32),
+                    in_=weight_scales[src].bitcast(I32)[g, 4 * quadrant : 4 * quadrant + 4, :].rearrange("r (j e n) -> e j r n", j=GATES, e=HALVES)[half],
                 )
 
         w_words = {}
@@ -100,10 +101,10 @@ def tile_lstmcell_kernel(tc, x, h_tm1, c_tm1, input_weight_words, input_weight_s
 
         spread = {}
 
-        def spread_bias(n):
+        def spread_bias(n, pool):
             half, gate = divmod(n, GATES)
             j = gate * HALVES + half
-            spread[n] = psum.tile([P, BANK], F32, name="spread", tag="bank")
+            spread[n] = pool.tile([P, BANK], F32, name="spread", tag="bank")
             nc.tensor.matmul(spread[n][:], lhsT=identity_bf[:, j : j + 1].to_broadcast([P, P]), rhs=bias_rows[:], start=True, stop=True)
 
         def keep_bias(n, engine):
@@ -115,20 +116,24 @@ def tile_lstmcell_kernel(tc, x, h_tm1, c_tm1, input_weight_words, input_weight_s
 
         load_activations(0, 0, 2)
         nc.sync.dma_start(out=bias_rows[0 : GATES * HALVES, :], in_=bias.rearrange("(j n) -> j n", n=BANK))
-        load_scales(0, 0)
+        load_scales(0, 0, 0)
         load_activations(0, 2, 2)
-        load_scales(0, 1)
+        load_scales(0, 1, 0)
         load_weights(0, FORGET, 0)
         load_activations(1, 0, 2)
-        load_scales(1, 0)
         load_activations(1, 2, 2)
-        load_scales(1, 1)
+        load_weights(0, ENTER, 0)
+        load_scales(1, 0, 0)
+        load_scales(1, 1, 0)
         load_weights(1, FORGET, 0)
-        for gate in (ENTER, CAND, LEAVE):
+        load_weights(1, ENTER, 0)
+        load_cell(0)
+        for gate in (CAND, LEAVE):
             load_weights(0, gate, 0)
             load_weights(1, gate, 0)
-            if gate == ENTER:
-                load_cell(0)
+        for src in range(SOURCES):
+            for g in range(GROUPS):
+                load_scales(src, g, 1)
         load_cell(1)
         for gate in range(GATES):
             load_weights(0, gate, 1)
@@ -143,9 +148,9 @@ def tile_lstmcell_kernel(tc, x, h_tm1, c_tm1, input_weight_words, input_weight_s
         flipped = {}
         grouped = {}
 
-        def flip(src, m):
+        def flip(src, m, pool):
             words = rows_sb[src][:, m, :].bitcast(F32)
-            flipped[(src, m)] = psum.tile([P, GROUPS, 2, P], F32, name="flipped", tag="bank")
+            flipped[(src, m)] = pool.tile([P, GROUPS, 2, P], F32, name="flipped", tag="bank")
             for g in range(GROUPS):
                 for u in range(2):
                     nc.tensor.transpose(flipped[(src, m)][:, g, u, :], words[:, g * GROUP_WORDS + u : (g + 1) * GROUP_WORDS : 2], identity[:])
@@ -226,53 +231,44 @@ def tile_lstmcell_kernel(tc, x, h_tm1, c_tm1, input_weight_words, input_weight_s
         pieces.extend([(m, LEAVE, 1) for m in range(BATCH_TILES)])
 
         early = {}
-        flip(0, 0)
+        flip(0, 0, psum_a)
         regroup(0, 0, 0)
-        flip(0, 1)
+        flip(0, 1, psum_a)
         regroup(0, 1, 1)
         quantise(0, 0)
         quantise(0, 1)
-        spread_bias(0)
-        spread_bias(1)
-        spread_bias(2)
+        spread_bias(0, psum_a)
+        spread_bias(1, psum_a)
+        spread_bias(2, psum_b)
         keep_bias(0, 0)
         keep_bias(1, 0)
-        flip(0, 2)
+        flip(0, 2, psum_b)
         regroup(0, 2, 0)
-        flip(0, 3)
+        flip(0, 3, psum_b)
         regroup(0, 3, 1)
         quantise(0, 2)
         quantise(0, 3)
         keep_bias(2, 0)
-        for n in range(3, 8):
-            spread_bias(n)
+        spread_bias(3, psum_b)
+        for n in range(4, 8):
+            spread_bias(n, psum_a)
         keep_bias(3, 0)
         keep_bias(4, 0)
         keep_bias(5, 0)
         keep_bias(6, 1)
         keep_bias(7, 1)
         for m in range(BATCH_TILES):
-            early[m] = psum.tile([P, BANK], F32, name="acc", tag="bank")
-        for k in range(GROUPS):
-            mx_pass(early[0], 0, FORGET, 0, k)
-        for k in range(GROUPS):
-            mx_pass(early[1], 1, FORGET, 0, k)
-        flip(1, 0)
-        regroup(1, 0, 0)
-        quantise(1, 0)
-        flip(1, 1)
-        regroup(1, 1, 0)
-        quantise(1, 1)
-        flip(1, 2)
-        regroup(1, 2, 0)
-        quantise(1, 2)
-        flip(1, 3)
-        regroup(1, 3, 0)
-        quantise(1, 3)
-        for k in range(GROUPS):
-            mx_pass(early[2], 2, FORGET, 0, k)
-        for k in range(GROUPS):
-            mx_pass(early[3], 3, FORGET, 0, k)
+            early[m] = psum_b.tile([P, BANK], F32, name="acc", tag="bank")
+            for k in range(GROUPS):
+                mx_pass(early[m], m, FORGET, 0, k)
+        for m in range(BATCH_TILES):
+            flip(1, m, psum_a)
+            regroup(1, m, 0)
+            quantise(1, m)
+        for m in range(BATCH_TILES):
+            early[BATCH_TILES + m] = psum_a.tile([P, BANK], F32, name="acc", tag="bank")
+            for k in range(GROUPS):
+                mx_pass(early[BATCH_TILES + m], m, ENTER, 0, k)
 
         later = {}
         tanh_step = {}
@@ -284,10 +280,10 @@ def tile_lstmcell_kernel(tc, x, h_tm1, c_tm1, input_weight_words, input_weight_s
             if j < len(pieces):
                 m, gate, half = pieces[j]
                 if j < len(early):
-                    acc = early[m]
+                    acc = early[j]
                     passes_done = GROUPS
                 else:
-                    acc = psum.tile([P, BANK], F32, name="acc", tag="bank")
+                    acc = (psum_b, psum_a)[(j // BATCH_TILES) % 2].tile([P, BANK], F32, name="acc", tag="bank")
                     passes_done = 0
                 for k in range(passes_done, PASSES):
                     mx_pass(acc, m, gate, half, k)

@@ -298,8 +298,8 @@ def tile_lstmcell_kernel(tc, x, h_tm1, c_tm1, input_weight_words, input_weight_s
                     at(tanh_step[(m, half)], cell_tanh, m, half)
                 elif gate == CAND:
                     at(j + 2, enter_times_cand, m, half)
-                    at(j + 3, cell_sum, m, half, False)
-                    tanh_step[(m, half)] = j + 5
+                    at(j + 3, cell_sum, m, half, True)
+                    tanh_step[(m, half)] = j + 4
                     at(tanh_step[(m, half)], cell_tanh, m, half)
                 if gate == LEAVE:
                     at(max(j, tanh_step[(m, half)]) + 2, cell_output, m, half)

@@ -68,7 +68,7 @@ def tile_lstmcell_kernel(tc, x, h_tm1, c_tm1, input_weight_words, input_weight_s
         def load_activations(src, first, count):
             nc.sync.dma_start(
                 out=rows_sb[src][:, first : first + count, :],
-                in_=activations[src][first * P : (first + count) * P, :].rearrange("(m p) k -> p m k", p=P),
+                in_=activations[src].rearrange("(p m) k -> p m k", m=BATCH_TILES)[:, first : first + count, :],
             )
 
         def load_scales(src, g, half):
@@ -94,7 +94,7 @@ def tile_lstmcell_kernel(tc, x, h_tm1, c_tm1, input_weight_words, input_weight_s
             c_prev[half] = keep.tile([P, BATCH_TILES, BANK], BF16, name="c_prev%d" % half)
             nc.sync.dma_start(
                 out=c_prev[half][:],
-                in_=c_tm1[:, half * BANK : (half + 1) * BANK].rearrange("(m p) c -> p m c", p=P),
+                in_=c_tm1.rearrange("(p m) c -> p m c", m=BATCH_TILES)[:, :, half * BANK : (half + 1) * BANK],
             )
 
         bias_all = keep.tile([P, HALVES, GATES, BANK], F32)
@@ -211,7 +211,7 @@ def tile_lstmcell_kernel(tc, x, h_tm1, c_tm1, input_weight_words, input_weight_s
                 nc.vector.tensor_add(out=c_new[:], in0=gate_sb[(m, CAND, half)][:], in1=gate_sb[(m, FORGET, half)][:])
             else:
                 nc.gpsimd.tensor_tensor(out=c_new[:], in0=gate_sb[(m, CAND, half)][:], in1=gate_sb[(m, FORGET, half)][:], op=ADD)
-            nc.sync.dma_start(out=c_t[m * P : (m + 1) * P, half * BANK : (half + 1) * BANK], in_=c_new[:])
+            nc.sync.dma_start(out=c_t.rearrange("(p m) c -> p m c", m=BATCH_TILES)[:, m, half * BANK : (half + 1) * BANK], in_=c_new[:])
 
         def cell_tanh(m, half):
             tanh_c[(m, half)] = work.tile([P, BANK], F32, name="tanh_c")
@@ -220,7 +220,7 @@ def tile_lstmcell_kernel(tc, x, h_tm1, c_tm1, input_weight_words, input_weight_s
         def cell_output(m, half):
             h_new = work.tile([P, BANK], F32, name="h_new")
             nc.vector.tensor_mul(out=h_new[:], in0=gate_sb[(m, LEAVE, half)][:], in1=tanh_c[(m, half)][:])
-            nc.sync.dma_start(out=h_t[m * P : (m + 1) * P, half * BANK : (half + 1) * BANK], in_=h_new[:])
+            nc.sync.dma_start(out=h_t.rearrange("(p m) c -> p m c", m=BATCH_TILES)[:, m, half * BANK : (half + 1) * BANK], in_=h_new[:])
 
         pieces = [(m, FORGET, 0) for m in range(BATCH_TILES)]
         pieces.extend([(m, ENTER, 0) for m in range(BATCH_TILES)])

@@ -121,19 +121,21 @@ def tile_lstmcell_kernel(tc, x, h_tm1, c_tm1, input_weight_words, input_weight_s
         load_scales(0, 1, 0)
         load_weights(0, FORGET, 0)
         load_activations(1, 0, 2)
+        load_scales(1, 0, 0)
         load_activations(1, 2, 2)
         load_weights(0, ENTER, 0)
-        load_scales(1, 0, 0)
         load_scales(1, 1, 0)
         load_weights(1, FORGET, 0)
         load_weights(1, ENTER, 0)
         load_cell(0)
-        for gate in (CAND, LEAVE):
-            load_weights(0, gate, 0)
-            load_weights(1, gate, 0)
-        for src in range(SOURCES):
-            for g in range(GROUPS):
-                load_scales(src, g, 1)
+        load_weights(0, CAND, 0)
+        load_scales(0, 0, 1)
+        load_weights(1, CAND, 0)
+        load_scales(0, 1, 1)
+        load_weights(0, LEAVE, 0)
+        load_scales(1, 0, 1)
+        load_weights(1, LEAVE, 0)
+        load_scales(1, 1, 1)
         load_cell(1)
         for gate in range(GATES):
             load_weights(0, gate, 1)

@@ -50,9 +50,10 @@ def tile_lstmcell_kernel(tc, x, h_tm1, c_tm1, input_weight_words, input_weight_s
         ctx.enter_context(tc.manual_schedule())
 
         w_planes = keep.tile([P, PASSES, FEATURES], U8, align_bytes=256)
-        nc.vector.memset(w_planes[:].bitcast(I32), 0)
         bias_rows = keep.tile([P, BANK], BF16)
-        nc.gpsimd.memset(bias_rows[:], 0.0)
+        nc.vector.memset(bias_rows[:], 0.0)
+        nc.scalar.dma_start(out=bias_rows[0 : GATES * HALVES, :], in_=bias.rearrange("(j n) -> j n", n=BANK))
+        nc.vector.memset(w_planes[:].bitcast(I32), 0)
         identity_bf = keep.tile([P, P], BF16)
         make_identity(nc, identity_bf[:])
         identity = keep.tile([P, P], F32)
@@ -115,7 +116,6 @@ def tile_lstmcell_kernel(tc, x, h_tm1, c_tm1, input_weight_words, input_weight_s
                 nc.vector.tensor_copy(out=bias_all[:, half, gate, :], in_=spread[n][:])
 
         load_activations(0, 0, 2)
-        nc.sync.dma_start(out=bias_rows[0 : GATES * HALVES, :], in_=bias.rearrange("(j n) -> j n", n=BANK))
         load_scales(0, 0, 0)
         load_activations(0, 2, 2)
         load_scales(0, 1, 0)
@@ -233,28 +233,28 @@ def tile_lstmcell_kernel(tc, x, h_tm1, c_tm1, input_weight_words, input_weight_s
         pieces.extend([(m, LEAVE, 1) for m in range(BATCH_TILES)])
 
         early = {}
+        spread_bias(0, psum_a)
+        spread_bias(1, psum_a)
+        keep_bias(0, 0)
+        keep_bias(1, 1)
         flip(0, 0, psum_a)
         regroup(0, 0, 0)
         flip(0, 1, psum_a)
         regroup(0, 1, 1)
         quantise(0, 0)
         quantise(0, 1)
-        spread_bias(0, psum_a)
-        spread_bias(1, psum_a)
         spread_bias(2, psum_b)
-        keep_bias(0, 0)
-        keep_bias(1, 0)
+        spread_bias(3, psum_b)
+        keep_bias(2, 0)
+        keep_bias(3, 0)
         flip(0, 2, psum_b)
         regroup(0, 2, 0)
         flip(0, 3, psum_b)
         regroup(0, 3, 1)
         quantise(0, 2)
         quantise(0, 3)
-        keep_bias(2, 0)
-        spread_bias(3, psum_b)
         for n in range(4, 8):
             spread_bias(n, psum_a)
-        keep_bias(3, 0)
         keep_bias(4, 0)
         keep_bias(5, 0)
         keep_bias(6, 1)

@@ -290,13 +290,18 @@ def tile_lstmcell_kernel(tc, x, h_tm1, c_tm1, input_weight_words, input_weight_s
                 for k in range(passes_done, PASSES):
                     mx_pass(acc, m, gate, half, k)
                 activate(acc, m, gate, half)
-                last_cell = (m >= BATCH_TILES - 2 and half == HALVES - 1)
+                last_cell = (m == BATCH_TILES - 1 and half == HALVES - 1)
                 if gate == FORGET:
                     at(j + 2, forget_times_cell, m, half)
                 if gate == CAND and last_cell:
                     at(j + 1, enter_times_cand, m, half)
                     at(j + 2, cell_sum, m, half, True)
                     tanh_step[(m, half)] = j + 3
+                    at(tanh_step[(m, half)], cell_tanh, m, half)
+                elif gate == CAND and half == HALVES - 1 and m < BATCH_TILES - 2:
+                    at(j + 2, enter_times_cand, m, half)
+                    at(j + 3, cell_sum, m, half, False)
+                    tanh_step[(m, half)] = j + 5
                     at(tanh_step[(m, half)], cell_tanh, m, half)
                 elif gate == CAND:
                     at(j + 2, enter_times_cand, m, half)

from contextlib import ExitStack

import concourse.mybir as mybir
from concourse.masks import make_identity

F32 = mybir.dt.float32
BF16 = mybir.dt.bfloat16
I32 = mybir.dt.int32
U32 = mybir.dt.uint32
U8 = mybir.dt.uint8
FP8X4 = mybir.dt.float8_e4m3fn_x4
SIGMOID = mybir.ActivationFunctionType.Sigmoid
TANH = mybir.ActivationFunctionType.Tanh
MULT = mybir.AluOpType.mult
ADD = mybir.AluOpType.add

P = 128
BATCH = 512
FEATURES = 1024
FORGET, ENTER, CAND, LEAVE = 0, 1, 2, 3
GATES = 4
GATE_FUNC = (SIGMOID, SIGMOID, TANH, SIGMOID)
GATE_NAME = ("forget", "enter", "cand", "leave")
SOURCES = 2
GROUPS = 2
PASSES = SOURCES * GROUPS
BANK = 512
BATCH_TILES = BATCH // P
HALVES = FEATURES // BANK
GROUP_WORDS = 256
PLANE_ROWS = 4

FLOPS = 2 * BATCH * (SOURCES * FEATURES) * (GATES * FEATURES)


def tile_lstmcell_kernel(tc, x, h_tm1, c_tm1, input_weight_words, input_weight_scales,
                                       hidden_state_weight_words, hidden_state_weight_scales, bias, out_0, out_1):
    nc = tc.nc
    h_t, c_t = out_0, out_1
    activations = (x, h_tm1)
    weight_words = (input_weight_words, hidden_state_weight_words)
    weight_scales = (input_weight_scales, hidden_state_weight_scales)

    with ExitStack() as ctx:
        keep = ctx.enter_context(tc.tile_pool(name="keep", bufs=1))
        stage = ctx.enter_context(tc.tile_pool(name="stage", bufs=4))
        work = ctx.enter_context(tc.tile_pool(name="work", bufs=6))
        psum_a = ctx.enter_context(tc.psum_pool(name="psum_a", bufs=4))
        psum_b = ctx.enter_context(tc.psum_pool(name="psum_b", bufs=4))
        ctx.enter_context(tc.manual_schedule())

        w_planes = keep.tile([P, PASSES, FEATURES], U8, align_bytes=256)
        bias_rows = keep.tile([P, BANK], BF16)
        nc.vector.memset(bias_rows[:], 0.0)
        nc.scalar.dma_start(out=bias_rows[0 : GATES * HALVES, :], in_=bias.rearrange("(j n) -> j n", n=BANK))
        nc.vector.memset(w_planes[:].bitcast(I32), 0)
        identity_bf = keep.tile([P, P], BF16)
        make_identity(nc, identity_bf[:])
        identity = keep.tile([P, P], F32)
        make_identity(nc, identity[:])
        table_warmer = keep.tile([P, 1], F32)
        nc.vector.memset(table_warmer[:], 0.0)
        nc.scalar.activation(out=table_warmer[:], in_=table_warmer[:], func=SIGMOID)

        rows_sb = {}
        for src in range(SOURCES):
            rows_sb[src] = keep.tile([P, BATCH_TILES, FEATURES], BF16, name="rows%d" % src)

        def load_activations(src, first, count):
            nc.sync.dma_start(
                out=rows_sb[src][:, first : first + count, :],
                in_=activations[src].rearrange("(p m) k -> p m k", m=BATCH_TILES)[:, first : first + count, :],
            )

        def load_scales(src, g, half):
            for quadrant in range(4):
                nc.sync.dma_start(
                    out=w_planes[32 * quadrant : 32 * quadrant + 16, src * GROUPS + g, half * BANK : (half + 1) * BANK].bitcast(I32),
                    in_=weight_scales[src].bitcast(I32)[g, 4 * quadrant : 4 * quadrant + 4, :].rearrange("r (j e n) -> e j r n", j=GATES, e=HALVES)[half],
                )

        w_words = {}

        def load_weights(src, gate, half):
            first = gate * FEATURES + half * BANK
            w_words[(src, gate, half)] = keep.tile([P, GROUPS, BANK], U32, name="w%d_%d_%d" % (src, gate, half), align_bytes=256)
            nc.sync.dma_start(
                out=w_words[(src, gate, half)][:].bitcast(I32),
                in_=weight_words[src].rearrange("g p n t -> p g (n t)").bitcast(I32)[:, :, first : first + BANK],
            )

        c_prev = {}

        def load_cell(half):
            c_prev[half] = keep.tile([P, BATCH_TILES, BANK], BF16, name="c_prev%d" % half)
            nc.sync.dma_start(
                out=c_prev[half][:],
                in_=c_tm1.rearrange("(p m) c -> p m c", m=BATCH_TILES)[:, :, half * BANK : (half + 1) * BANK],
            )

        bias_all = keep.tile([P, HALVES, GATES, BANK], F32)

        spread = {}

        def spread_bias(n, pool):
            half, gate = divmod(n, GATES)
            j = gate * HALVES + half
            spread[n] = pool.tile([P, BANK], F32, name="spread", tag="bank")
            nc.tensor.matmul(spread[n][:], lhsT=identity_bf[:, j : j + 1].to_broadcast([P, P]), rhs=bias_rows[:], start=True, stop=True)

        def keep_bias(n, engine):
            half, gate = divmod(n, GATES)
            if engine == 0:
                nc.scalar.copy(out=bias_all[:, half, gate, :], in_=spread[n][:])
            else:
                nc.vector.tensor_copy(out=bias_all[:, half, gate, :], in_=spread[n][:])

        load_activations(0, 0, 2)
        load_scales(0, 0, 0)
        load_activations(0, 2, 2)
        load_scales(0, 1, 0)
        load_weights(0, FORGET, 0)
        load_activations(1, 0, 2)
        load_scales(1, 0, 0)
        load_activations(1, 2, 2)
        load_weights(0, ENTER, 0)
        load_scales(1, 1, 0)
        load_weights(1, FORGET, 0)
        load_weights(1, ENTER, 0)
        load_cell(0)
        load_weights(0, CAND, 0)
        load_scales(0, 0, 1)
        load_weights(1, CAND, 0)
        load_scales(0, 1, 1)
        load_weights(0, LEAVE, 0)
        load_scales(1, 0, 1)
        load_weights(1, LEAVE, 0)
        load_scales(1, 1, 1)
        load_cell(1)
        for gate in range(GATES):
            load_weights(0, gate, 1)
            load_weights(1, gate, 1)

        a_codes = {}
        a_scales = {}
        for src in range(SOURCES):
            a_codes[src] = keep.tile([P, BATCH_TILES, GROUPS, P], U32, name="a_codes%d" % src, align_bytes=256)
            a_scales[src] = keep.tile([P, BATCH_TILES, GROUPS, P], U8, name="a_scales%d" % src, align_bytes=256)

        flipped = {}
        grouped = {}

        def flip(src, m, pool):
            words = rows_sb[src][:, m, :].bitcast(F32)
            flipped[(src, m)] = pool.tile([P, GROUPS, 2, P], F32, name="flipped", tag="bank")
            for g in range(GROUPS):
                for u in range(2):
                    nc.tensor.transpose(flipped[(src, m)][:, g, u, :], words[:, g * GROUP_WORDS + u : (g + 1) * GROUP_WORDS : 2], identity[:])

        def regroup(src, m, engine):
            grouped[(src, m)] = stage.tile([P, GROUPS * P * 4], BF16, name="grouped", align_bytes=256)
            out = grouped[(src, m)][:].bitcast(F32).rearrange("p (g b u) -> p g b u", g=GROUPS, u=2)
            in_ = flipped[(src, m)][:].rearrange("p g u b -> p g b u")
            if engine == 0:
                nc.scalar.copy(out=out, in_=in_)
            else:
                nc.vector.tensor_copy(out=out, in_=in_)

        def quantise(src, m):
            nc.vector.quantize_mx(
                out=a_codes[src][:, m, :, :].rearrange("p g b -> p (g b)").bitcast(FP8X4),
                scales=a_scales[src][:, m, :, :].rearrange("p g b -> p (g b)"),
                in_=grouped[(src, m)][:],
            )


        def mx_pass(acc, m, gate, half, k):
            src, g = divmod(k, GROUPS)
            first = gate * FEATURES + half * BANK
            nc.tensor.matmul_mx(
                out=acc[:],
                lhsT=a_codes[src][:, m, g, :].bitcast(FP8X4),
                lhsT_scale=a_scales[src][:, m, g, :],
                rhs=w_words[(src, gate, half)][:, g, :].bitcast(FP8X4),
                rhs_scale=w_planes[PLANE_ROWS * gate : P, k, half * BANK : (half + 1) * BANK],
                start=(k == 0),
                stop=(k == PASSES - 1),
            )

        gate_sb = {}
        tanh_c = {}

        def activate(acc, m, gate, half):
            value = work.tile([P, BANK], F32, name="value", tag=GATE_NAME[gate])
            nc.vector.tensor_add(out=value[:], in0=acc[:], in1=bias_all[:, half, gate, :])
            nc.scalar.activation(out=value[:], in_=value[:], func=GATE_FUNC[gate])
            gate_sb[(m, gate, half)] = value

        def forget_times_cell(m, half):
            value = gate_sb[(m, FORGET, half)]
            nc.gpsimd.tensor_tensor(out=value[:], in0=value[:], in1=c_prev[half][:, m, :], op=MULT)

        def enter_times_cand(m, half):
            value = gate_sb[(m, CAND, half)]
            nc.vector.tensor_mul(out=value[:], in0=value[:], in1=gate_sb[(m, ENTER, half)][:])

        c_sb = {}

        def cell_sum(m, half, on_vector):
            c_new = work.tile([P, BANK], F32, name="c_new")
            c_sb[(m, half)] = c_new
            if on_vector:
                nc.vector.tensor_add(out=c_new[:], in0=gate_sb[(m, CAND, half)][:], in1=gate_sb[(m, FORGET, half)][:])
            else:
                nc.gpsimd.tensor_tensor(out=c_new[:], in0=gate_sb[(m, CAND, half)][:], in1=gate_sb[(m, FORGET, half)][:], op=ADD)
            nc.sync.dma_start(out=c_t.rearrange("(p m) c -> p m c", m=BATCH_TILES)[:, m, half * BANK : (half + 1) * BANK], in_=c_new[:])

        def cell_tanh(m, half):
            tanh_c[(m, half)] = work.tile([P, BANK], F32, name="tanh_c")
            nc.scalar.activation(out=tanh_c[(m, half)][:], in_=c_sb[(m, half)][:], func=TANH)

        def cell_output(m, half):
            h_new = work.tile([P, BANK], F32, name="h_new")
            nc.vector.tensor_mul(out=h_new[:], in0=gate_sb[(m, LEAVE, half)][:], in1=tanh_c[(m, half)][:])
            nc.sync.dma_start(out=h_t.rearrange("(p m) c -> p m c", m=BATCH_TILES)[:, m, half * BANK : (half + 1) * BANK], in_=h_new[:])

        pieces = [(m, FORGET, 0) for m in range(BATCH_TILES)]
        pieces.extend([(m, ENTER, 0) for m in range(BATCH_TILES)])
        pieces.extend([(m, CAND, 0) for m in range(BATCH_TILES)])
        pieces.extend([(m, LEAVE, 0) for m in range(BATCH_TILES)])
        pieces.extend([(m, FORGET, 1) for m in range(BATCH_TILES)])
        pieces.extend([(m, gate, 1) for m in range(BATCH_TILES) for gate in (ENTER, CAND)])
        pieces.extend([(m, LEAVE, 1) for m in range(BATCH_TILES)])

        early = {}
        spread_bias(0, psum_a)
        spread_bias(1, psum_a)
        keep_bias(0, 0)
        keep_bias(1, 1)
        flip(0, 0, psum_a)
        regroup(0, 0, 0)
        flip(0, 1, psum_a)
        regroup(0, 1, 1)
        quantise(0, 0)
        quantise(0, 1)
        spread_bias(2, psum_b)
        spread_bias(3, psum_b)
        keep_bias(2, 0)
        keep_bias(3, 0)
        flip(0, 2, psum_b)
        regroup(0, 2, 0)
        flip(0, 3, psum_b)
        regroup(0, 3, 1)
        quantise(0, 2)
        quantise(0, 3)
        for n in range(4, 8):
            spread_bias(n, psum_a)
        keep_bias(4, 0)
        keep_bias(5, 0)
        keep_bias(6, 1)
        keep_bias(7, 1)
        for m in range(BATCH_TILES):
            early[m] = psum_b.tile([P, BANK], F32, name="acc", tag="bank")
            for k in range(GROUPS):
                mx_pass(early[m], m, FORGET, 0, k)
        for m in range(BATCH_TILES):
            flip(1, m, psum_a)
            regroup(1, m, 0)
            quantise(1, m)
        for m in range(BATCH_TILES):
            early[BATCH_TILES + m] = psum_a.tile([P, BANK], F32, name="acc", tag="bank")
            for k in range(GROUPS):
                mx_pass(early[BATCH_TILES + m], m, ENTER, 0, k)

        later = {}
        tanh_step = {}

        def at(step, action, *args):
            later.setdefault(step, []).append((action, args))

        for j in range(len(pieces) + 4):
            if j < len(pieces):
                m, gate, half = pieces[j]
                if j < len(early):
                    acc = early[j]
                    passes_done = GROUPS
                else:
                    acc = (psum_b, psum_a)[(j // BATCH_TILES) % 2].tile([P, BANK], F32, name="acc", tag="bank")
                    passes_done = 0
                for k in range(passes_done, PASSES):
                    mx_pass(acc, m, gate, half, k)
                activate(acc, m, gate, half)
                last_cell = (m == BATCH_TILES - 1 and half == HALVES - 1)
                if gate == FORGET:
                    at(j + 2, forget_times_cell, m, half)
                if gate == CAND and last_cell:
                    at(j + 1, enter_times_cand, m, half)
                    at(j + 2, cell_sum, m, half, True)
                    tanh_step[(m, half)] = j + 3
                    at(tanh_step[(m, half)], cell_tanh, m, half)
                elif gate == CAND and half == HALVES - 1 and m < BATCH_TILES - 2:
                    at(j + 2, enter_times_cand, m, half)
                    at(j + 3, cell_sum, m, half, False)
                    tanh_step[(m, half)] = j + 5
                    at(tanh_step[(m, half)], cell_tanh, m, half)
                elif gate == CAND:
                    at(j + 2, enter_times_cand, m, half)
                    at(j + 3, cell_sum, m, half, True)
                    tanh_step[(m, half)] = j + 4
                    at(tanh_step[(m, half)], cell_tanh, m, half)
                if gate == LEAVE:
                    at(max(j, tanh_step[(m, half)]) + 2, cell_output, m, half)
            for action, args in later.get(j, []):
                action(*args)
